import numpy as np
import ml_dtypes


def mxq(x, axis, fmt="e4m3"):
    dtype, down = {"e4m3": (ml_dtypes.float8_e4m3fn, 7), "e5m2": (ml_dtypes.float8_e5m2, 14)}[fmt]
    v = np.moveaxis(np.asarray(x, np.float32).astype(ml_dtypes.bfloat16).astype(np.float64), axis, -1)
    blocks = v.reshape(v.shape[:-1] + (-1, 32))
    amax = np.abs(blocks).max(-1, keepdims=True)
    byte = np.maximum(np.where(amax > 0, np.frexp(amax)[1] - 1 + 127, 0) - down, 1)
    scale = np.exp2(byte - 127.0)
    codes = (blocks / scale).astype(np.float32).astype(dtype).astype(np.float64)
    return np.moveaxis((codes * scale).reshape(v.shape), -1, axis)


WIDE = False


def mx_kscale(k):
    if not WIDE:
        return np.ones(k)
    levels = np.array([18, -18])
    if k % 512:
        return np.exp2(np.random.permutation(np.resize(levels, k // 32))).repeat(32)
    a = np.empty((k // 512, 16))
    for p in range(k // 512):
        a[p, :8] = np.random.permutation(np.resize(levels, 8))
        for g in range(8):
            far = levels[np.abs(levels - a[p, g]) >= 10]
            a[p, g + 8] = far[np.random.randint(len(far))]
    return np.exp2(a.ravel()).repeat(32)


BF16 = ml_dtypes.bfloat16


def bf(x):
    return np.asarray(x, np.float32).astype(BF16)


def f64(x):
    return np.asarray(x).astype(np.float64)


B, D, E, NM = 512, 1024, 1024, 4


def setup_inputs():
    s = mx_kscale(B)[:, None]
    uj = mx_kscale(NM * E)[::NM]
    u = np.repeat(uj, NM)
    v = mx_kscale(D)
    gain = np.ones((E, NM))
    gain[:, 1] = 0.3
    off = np.zeros((E, NM))
    off[:, 1] = 1.3 * np.sign(np.random.standard_normal(E))
    a0 = bf(np.maximum(np.random.standard_normal((B, D)) * 1.2, 0.0))
    w1_0 = bf(np.random.standard_normal((D, D)) / np.sqrt(D))
    b1 = bf(np.random.standard_normal(D) * 0.2)
    w2_0 = bf(np.random.standard_normal((D, NM * E)) / np.sqrt(D) * gain.reshape(-1))
    b2 = bf(np.random.standard_normal(NM * E) * 0.1 + off.reshape(-1))
    dopamine = bf(np.random.standard_normal((B, E)))
    serotonin = bf(np.random.standard_normal((B, E)))
    glutamate = bf(np.random.standard_normal((B, E)))
    gaba = bf(np.random.standard_normal((B, E)))
    g = np.random.standard_normal((NM, B, E)) * np.exp2(np.random.randint(-6, 1, (1, B, 1))) * 2.0
    g = bf((g / s * uj).reshape(NM * B, E))
    z1 = f64(a0) @ f64(w1_0) + f64(b1)
    h = np.tanh(np.maximum(z1, 0.0) @ f64(w2_0) + f64(b2))
    return {
        "prev_act": bf(f64(a0) * s),
        "W1": bf(f64(w1_0) / v),
        "b1": b1,
        "W2": bf(f64(w2_0) * v[:, None] / u),
        "b2": b2,
        "dopamine": dopamine,
        "serotonin": serotonin,
        "glutamate": glutamate,
        "gaba": gaba,
        "z1": np.asarray(z1, np.float32),
        "h": np.asarray(h, np.float32),
        "grad_out": g,
    }


def reference(prev_act, W1, b1, W2, b2, dopamine, serotonin, glutamate, gaba, z1, h, grad_out):
    hf = f64(h)
    preds = hf.reshape(B, E, NM)
    p_dop, p_ser, p_glu, p_gab = preds[..., 0], preds[..., 1], preds[..., 2], preds[..., 3]
    g = f64(grad_out).reshape(NM, B, E)
    g_dop, g_ser, g_glu, g_gab = g[0], g[1], g[2], g[3]
    a = np.abs(p_ser)
    inv = 1.0 / np.maximum(a, 1e-6)
    dinv = -np.sign(p_ser) * (a > 1e-6) * inv * inv
    d_ser = g_ser + (g_dop * p_dop + g_glu * p_glu + g_gab * p_gab) * dinv
    dpred = np.stack([g_dop * inv, d_ser, g_glu * inv, g_gab * inv], axis=-1).reshape(B, NM * E)
    dz2 = dpred * (1.0 - hf * hf)
    dhid = mxq(dz2, 1, "e5m2") @ mxq(f64(W2), 1, "e4m3").T
    dz1 = dhid * (f64(z1) > 0.0)
    dx = mxq(dz1, 1, "e5m2") @ mxq(f64(W1), 1, "e4m3").T
    dw1 = mxq(f64(prev_act), 0, "e4m3").T @ mxq(dz1, 0, "e5m2")
    return dx, dw1

@@ -1,0 +1,356 @@
+from contextlib import ExitStack
+
+import concourse.mybir as mybir
+from concourse.masks import make_identity
+
+B, D, E, NM = 512, 1024, 1024, 4
+
+FLOPS = 2 * B * D * NM * E + 2 * (2 * B * D * D)
+BYTES = 2 * (B * D + D * D + D * NM * E + NM * B * E) + 4 * (B * D + B * NM * E + B * D + D * D)
+
+F32 = mybir.dt.float32
+BF16 = mybir.dt.bfloat16
+U32 = mybir.dt.uint32
+U8 = mybir.dt.uint8
+E4 = mybir.dt.float8_e4m3fn_x4
+E5 = mybir.dt.float8_e5m2_x4
+ALU = mybir.AluOpType
+ACT = mybir.ActivationFunctionType
+
+P = 128
+J = 256
+NCH = B * E // (P * J)
+ORDER = (1, 0, 3, 2)
+
+
+def tile_hebbianlayer_pb_v_kernel(tc, prev_act, W1, b1, W2, b2, dopamine, serotonin, glutamate, gaba, z1, h, grad_out, out_0, out_1):
+    nc = tc.nc
+    prev_v = prev_act.rearrange("(p j) d -> p j d", j=4)
+    h_v = h.rearrange("(p j) k -> p j k", j=4)
+    z1_v = z1.rearrange("(p j) d -> p j d", j=4)
+    g_v = grad_out.rearrange("(c p j) e -> p c j e", c=4, j=4)
+    w2_v = W2.rearrange("(n b r) k -> r n b k", n=2, b=4)
+    w1_v = W1.rearrange("(n b r) k -> r n b k", n=2, b=4)
+    o0_v = out_0.rearrange("(p j) d -> p j d", j=4)
+
+    with ExitStack() as ctx:
+        keep = ctx.enter_context(tc.tile_pool(name="keep", bufs=1))
+        work = ctx.enter_context(tc.tile_pool(name="work", bufs=2))
+        psum = ctx.enter_context(tc.psum_pool(name="psum", bufs=2))
+        ctx.enter_context(tc.manual_schedule())
+
+        ident_b = keep.tile([P, P], BF16, name="ident_b")
+        ident_f = keep.tile([P, P], F32, name="ident_f")
+        eps = keep.tile([P, 1], F32, name="eps")
+        warm = keep.tile([P, 1], F32, name="warm")
+        nc.vector.memset(eps[:], 1e-25)
+        make_identity(nc, ident_b[:])
+        make_identity(nc, ident_f[:])
+        nc.scalar.activation(warm[:], eps[:], ACT.Abs_reciprocal_sqrt)
+
+        w2_codes = [keep.tile([P, 8, 512], U32, name="w2c%d" % n, align_bytes=64) for n in range(2)]
+        w2_scales = [keep.tile([P, 8, 512], U8, name="w2s%d" % n, align_bytes=64) for n in range(2)]
+        w1_codes = [keep.tile([P, 2, 512], U32, name="w1c%d" % n, align_bytes=64) for n in range(2)]
+        w1_scales = [keep.tile([P, 2, 512], U8, name="w1s%d" % n, align_bytes=64) for n in range(2)]
+        pv_codes = keep.tile([P, D], U32, name="pv_codes", align_bytes=64)
+        pv_scales = keep.tile([P, D], U8, name="pv_scales", align_bytes=64)
+        dz1 = keep.tile([P, 4, D], BF16, name="dz1", align_bytes=64)
+        t1_codes = keep.tile([P, D], U32, name="t1_codes", align_bytes=64)
+        t1_scales = keep.tile([P, D], U8, name="t1_scales", align_bytes=64)
+
+        hs, gs, ws, z1s = {}, {}, {}, {}
+        h2s, invs, inv2s, gps, xs, ys, ss, ts, os_ = {}, {}, {}, {}, {}, {}, {}, {}, {}
+        wg, dzg, dz2c, dz2s, acc, d1c = {}, {}, {}, {}, {}, {}
+
+        def load_h(i):
+            if i < NCH:
+                hs[i] = work.tile([P, J, 4], F32, name="h", tag="h", bufs=5, align_bytes=64)
+                nc.sync.dma_start(out=hs[i][:].rearrange("p j c -> p (j c)"), in_=h_v[:, i // 4, (i % 4) * 4 * J : (i % 4 + 1) * 4 * J])
+
+        def load_g(k):
+            if k < NCH // 2:
+                gs[k] = work.tile([P, 4, 2 * J], BF16, name="g", tag="g", bufs=2, align_bytes=64)
+                nc.sync.dma_start(out=gs[k][:], in_=g_v[:, :, k // 2, (k % 2) * 2 * J : (k % 2 + 1) * 2 * J])
+
+        def load_w(k):
+            if k < 10:
+                ws[k] = work.tile([P, 4, 1024], BF16, name="wraw", tag="wraw", bufs=3, align_bytes=64)
+                src = w2_v[:, k // 4, :, (k % 4) * 1024 : (k % 4 + 1) * 1024] if k < 8 else w1_v[:, k - 8, :, :]
+                nc.sync.dma_start(out=ws[k][:], in_=src)
+
+        def load_z1(t):
+            z1s[t] = work.tile([P, D], F32, name="z1t", tag="z1t", bufs=2, align_bytes=64)
+            nc.sync.dma_start(out=z1s[t][:], in_=z1_v[:, t, :])
+
+        def w_transposes(k, gg, half):
+            xt = psum.tile([P, 2, 2, P], F32, name="xt", tag="w", bufs=2)
+            words = ws[k][:].bitcast(F32)
+            for bb in range(2):
+                for u in range(2):
+                    nc.tensor.transpose(xt[:, bb, u, :], words[:, 2 * half + bb, 256 * gg + u : 256 * (gg + 1) : 2], ident_f[:])
+            return xt
+
+        def w_copy(k, gg, half, xt):
+            if half == 0:
+                wg[k, gg] = work.tile([P, 4, P, 4], BF16, name="wg", tag="wg", bufs=3, align_bytes=64)
+            dst = wg[k, gg][:].bitcast(F32)
+            nc.scalar.copy(dst[:, 2 * half : 2 * half + 2, :, :], xt[:].rearrange("p b u r -> p b r u"))
+
+        def w_quant(k, gg):
+            if k < 0 or k > 9:
+                return
+            if k < 8:
+                g, co, sc = 2 * (k % 4) + gg, w2_codes[k // 4], w2_scales[k // 4]
+            else:
+                g, co, sc = gg, w1_codes[k - 8], w1_scales[k - 8]
+            nc.vector.quantize_mx(out=co[:, g, :].bitcast(E4), scales=sc[:, g, :], in_=wg[k, gg][:].rearrange("p b r t -> p (b r t)"))
+
+        def sc_square(i):
+            h2s[i] = work.tile([P, J, 4], F32, name="h2", tag="h2", bufs=4, align_bytes=64)
+            nc.scalar.activation(h2s[i][:].rearrange("p j c -> p (j c)"), hs[i][:].rearrange("p j c -> p (j c)"), ACT.Square)
+
+        def sc_inv(i):
+            invs[i] = work.tile([P, J], F32, name="inv", tag="inv", bufs=3, align_bytes=64)
+            nc.scalar.activation(invs[i][:], h2s[i][:, :, 1], ACT.Abs_reciprocal_sqrt, bias=eps[:])
+
+        def sc_inv2(i):
+            inv2s[i] = work.tile([P, J], F32, name="inv2", tag="inv2", bufs=3, align_bytes=64)
+            nc.scalar.activation(inv2s[i][:], invs[i][:], ACT.Square)
+
+        def pe_g(i):
+            gps[i] = psum.tile([P, 4, J], BF16, name="gp", tag="g", bufs=3)
+            for pos in range(4):
+                nc.tensor.matmul(gps[i][:, pos, :], lhsT=ident_b[:], rhs=gs[i // 2][:, ORDER[pos], (i % 2) * J : (i % 2 + 1) * J], start=True, stop=True)
+
+        def v_x(i):
+            xs[i] = work.tile([P, 4, J], F32, name="x", tag="x", bufs=3, align_bytes=64)
+            nc.vector.scalar_tensor_tensor(out=xs[i][:, 1:4, :], in0=invs[i][:].unsqueeze(1).to_broadcast([P, 3, J]), scalar=1e6, in1=gps[i][:, 1:4, :], op0=ALU.min, op1=ALU.mult)
+
+        def v_m(i):
+            nc.vector.scalar_tensor_tensor(out=xs[i][:, 0, :], in0=invs[i][:], scalar=1e6, in1=inv2s[i][:], op0=ALU.is_lt, op1=ALU.mult)
+
+        def x_pairs(i):
+            return xs[i][:].rearrange("p (a e) j -> p a j e", e=2)[:, :, :, ::-1]
+
+        def v_y(i):
+            ys[i] = work.tile([P, 4, J], F32, name="y", tag="y", bufs=2, align_bytes=64)
+            nc.vector.tensor_tensor(out=ys[i][:].rearrange("p (a e) j -> p a j e", e=2), in0=hs[i][:].rearrange("p j (a e) -> p a j e", e=2), in1=x_pairs(i), op=ALU.mult)
+
+        def g_s(i):
+            s1 = work.tile([P, J], F32, name="s1", tag="s1", bufs=2, align_bytes=64)
+            ss[i] = work.tile([P, J], F32, name="s", tag="s", bufs=2, align_bytes=64)
+            nc.gpsimd.tensor_tensor(out=s1[:], in0=ys[i][:, 0, :], in1=ys[i][:, 2, :], op=ALU.add)
+            nc.gpsimd.tensor_tensor(out=ss[i][:], in0=s1[:], in1=ys[i][:, 3, :], op=ALU.add)
+
+        def v_t(i):
+            ts[i] = work.tile([P, J], F32, name="t", tag="t", bufs=2, align_bytes=64)
+            nc.vector.tensor_tensor(out=ts[i][:], in0=ys[i][:, 1, :], in1=ss[i][:], op=ALU.mult)
+
+        def v_d1(i):
+            nc.vector.tensor_tensor(out=xs[i][:, 0, :], in0=gps[i][:, 0, :], in1=ts[i][:], op=ALU.subtract)
+
+        def v_o(i):
+            os_[i] = work.tile([P, 2, J, 2], BF16, name="o", tag="o", bufs=3, align_bytes=64)
+            h2p = h2s[i][:].rearrange("p j (a e) -> p a j e", e=2)
+            xp = x_pairs(i)
+            for a in range(2):
+                nc.vector.scalar_tensor_tensor(out=os_[i][:, a, :, :], in0=h2p[:, a, :, :], scalar=1.0, in1=xp[:, a, :, :], op0=ALU.subtract, op1=ALU.mult)
+
+        def dz_transposes(i):
+            xt = psum.tile([P, 2, 2, P], F32, name="dzt", tag="dz", bufs=1)
+            words = os_[i][:].rearrange("p a j e -> p (a j e)").bitcast(F32)
+            for gg in range(2):
+                for a in range(2):
+                    nc.tensor.transpose(xt[:, gg, a, :], words[:, a * J + gg * P : a * J + (gg + 1) * P], ident_f[:])
+            dzg[i] = work.tile([P, 2, P, 4], BF16, name="dzg", tag="dzg", bufs=2, align_bytes=64)
+            nc.scalar.copy(dzg[i][:].bitcast(F32), xt[:].rearrange("p g a r -> p g r a"))
+
+        def dz_quant(i):
+            t, u = i // 4, i % 4
+            if u == 0:
+                dz2c[t] = work.tile([P, 8, P], U32, name="dz2c", tag="dz2c", bufs=2, align_bytes=64)
+                dz2s[t] = work.tile([P, 8, P], U8, name="dz2s", tag="dz2s", bufs=2, align_bytes=64)
+            nc.vector.quantize_mx(
+                out=dz2c[t][:, 2 * u : 2 * u + 2, :].rearrange("p g r -> p (g r)").bitcast(E5),
+                scales=dz2s[t][:, 2 * u : 2 * u + 2, :].rearrange("p g r -> p (g r)"),
+                in_=dzg[i][:].rearrange("p g r t -> p (g r t)"),
+            )
+
+        def mm_dhid(t, n, g):
+            if g == 0:
+                acc[t, n] = psum.tile([P, 512], F32, name="acc", tag="acc", bufs=2)
+            nc.tensor.matmul_mx(out=acc[t, n][:], lhsT=dz2c[t][:, g, :].bitcast(E5), lhsT_scale=dz2s[t][:, g, :], rhs=w2_codes[n][:, g, :].bitcast(E4), rhs_scale=w2_scales[n][:, g, :], start=(g == 0), stop=(g == 7))
+
+        def v_mask(t, n):
+            nc.vector.scalar_tensor_tensor(out=dz1[:, t, 512 * n : 512 * (n + 1)], in0=z1s[t][:, 512 * n : 512 * (n + 1)], scalar=0.0, in1=acc[t, n][:], op0=ALU.is_gt, op1=ALU.mult)
+
+        def dz1_transposes(t, copy):
+            xt = psum.tile([P, 2, 2, P], F32, name="d1t", tag="w", bufs=2)
+            words = dz1[:, t, :].bitcast(F32)
+            for g in range(2):
+                for u in range(2):
+                    nc.tensor.transpose(xt[:, g, u, :], words[:, 256 * g + u : 256 * (g + 1) : 2], ident_f[:])
+            grp = work.tile([P, 2, P, 4], BF16, name="d1g", tag="d1g", bufs=2, align_bytes=64)
+            copy(grp[:].bitcast(F32), xt[:].rearrange("p g u r -> p g r u"))
+            return grp
+
+        def dz1_quant(t, grp):
+            co = work.tile([P, 2, P], U32, name="d1c", tag="d1c", bufs=2, align_bytes=64)
+            sc = work.tile([P, 2, P], U8, name="d1s", tag="d1s", bufs=2, align_bytes=64)
+            nc.vector.quantize_mx(out=co[:].rearrange("p g r -> p (g r)").bitcast(E5), scales=sc[:].rearrange("p g r -> p (g r)"), in_=grp[:].rearrange("p g r t -> p (g r t)"))
+            d1c[t] = (co, sc)
+
+        def s_neg(dst, src):
+            nc.scalar.activation(dst, src, ACT.Copy, scale=-1.0)
+
+        def v_neg(dst, src):
+            nc.vector.tensor_scalar(out=dst, in0=src, scalar1=-1.0, scalar2=None, op0=ALU.mult)
+
+        def dx(t, engines):
+            co, sc = d1c[t]
+            ost = work.tile([P, D], F32, name="ost", tag="ost", bufs=2, align_bytes=64)
+            for n in range(2):
+                ps = psum.tile([P, 512], F32, name="dxp", tag="w", bufs=2)
+                for g in range(2):
+                    nc.tensor.matmul_mx(out=ps[:], lhsT=co[:, g, :].bitcast(E5), lhsT_scale=sc[:, g, :], rhs=w1_codes[n][:, g, :].bitcast(E4), rhs_scale=w1_scales[n][:, g, :], start=(g == 0), stop=(g == 1))
+                engines[n](ost[:, 512 * n : 512 * (n + 1)], ps[:])
+            nc.sync.dma_start(out=o0_v[:, t, :], in_=ost[:])
+
+        pv = work.tile([P, 4, 1024], BF16, name="wraw", tag="wraw", bufs=3, align_bytes=64)
+        for k in range(2):
+            nc.sync.dma_start(out=pv[:, :, 512 * k : 512 * (k + 1)], in_=prev_v[:, :, 512 * k : 512 * (k + 1)])
+        load_h(0)
+        load_g(0)
+        load_h(1)
+        load_w(0)
+        load_h(2)
+        load_g(1)
+        load_w(1)
+        load_h(3)
+
+        pvg = work.tile([P, D, 4], BF16, name="tok", tag="tok", bufs=1, align_bytes=64)
+        for k in range(2):
+            cols = slice(512 * k, 512 * (k + 1))
+            nc.vector.tensor_copy(out=pvg[:, cols, :], in_=pv[:, :, cols].rearrange("p j d -> p d j"))
+        for k in range(2):
+            cols = slice(512 * k, 512 * (k + 1))
+            nc.vector.quantize_mx(out=pv_codes[:, cols].bitcast(E4), scales=pv_scales[:, cols], in_=pvg[:, cols, :].rearrange("p d j -> p (d j)"))
+
+        for i in range(2):
+            sc_square(i)
+            sc_inv(i)
+            sc_inv2(i)
+            pe_g(i)
+        v_x(0)
+        v_m(0)
+
+        for i in range(NCH):
+            load_w(i + 2)
+            load_h(i + 4)
+            if i % 2 == 0:
+                load_g(i // 2 + 2)
+            if i in (5, 6, 10, 12):
+                load_z1({5: 0, 6: 1, 10: 2, 12: 3}[i])
+
+            if i >= 2:
+                dz_transposes(i - 2)
+            v_y(i)
+            g_s(i)
+            if i + 2 < NCH:
+                sc_square(i + 2)
+            if i < 10:
+                xa = w_transposes(i, 0, 0)
+                w_copy(i, 0, 0, xa)
+            if i + 2 < NCH:
+                sc_inv(i + 2)
+            if i < 10:
+                xa = w_transposes(i, 0, 1)
+                w_copy(i, 0, 1, xa)
+            if i + 2 < NCH:
+                sc_inv2(i + 2)
+            if i + 1 < NCH:
+                v_x(i + 1)
+            if i >= 1:
+                v_d1(i - 1)
+            if i + 2 < NCH:
+                pe_g(i + 2)
+            if i < 10:
+                for half in range(2):
+                    xa = w_transposes(i, 1, half)
+                    w_copy(i, 1, half, xa)
+            if i + 1 < NCH:
+                v_m(i + 1)
+            w_quant(i - 1, 1)
+            if i >= 1:
+                v_o(i - 1)
+            if i >= 2:
+                dz_quant(i - 2)
+            if i == 9:
+                v_mask(0, 0)
+                v_mask(0, 1)
+            if i == 10:
+                v_mask(1, 0)
+                v_mask(1, 1)
+            if i == 14:
+                v_mask(2, 0)
+                v_mask(2, 1)
+            w_quant(i, 0)
+            v_t(i)
+
+            if i == 8 or i == 9 or i == 13:
+                t = {8: 0, 9: 1, 13: 2}[i]
+                for n in range(2):
+                    for g in range(8):
+                        mm_dhid(t, n, g)
+            if i == 14 or i == 15:
+                for g in (2 * (i - 14), 2 * (i - 14) + 1):
+                    for n in range(2):
+                        mm_dhid(3, n, g)
+            if i in (11, 12, 15):
+                t = {11: 0, 12: 1, 15: 2}[i]
+                grp = dz1_transposes(t, nc.scalar.copy)
+                dz1_quant(t, grp)
+                dx(t, (s_neg, s_neg))
+
+        dz_transposes(NCH - 2)
+        v_d1(NCH - 1)
+        dz_quant(NCH - 2)
+        v_o(NCH - 1)
+        for g in (4, 5):
+            for n in range(2):
+                mm_dhid(3, n, g)
+        dz_transposes(NCH - 1)
+        dz_quant(NCH - 1)
+        for n in range(2):
+            for g in (6, 7):
+                mm_dhid(3, n, g)
+        v_mask(3, 0)
+        v_mask(3, 1)
+        tok = work.tile([P, D, 4], BF16, name="tok", tag="tok", bufs=1, align_bytes=64)
+        nc.vector.tensor_copy(out=tok[:, 0:512, :], in_=dz1[:, :, 0:512].rearrange("p j d -> p d j"))
+        nc.scalar.copy(tok[:, 512:1024, :], dz1[:, :, 512:1024].rearrange("p j d -> p d j"))
+        grp3 = dz1_transposes(3, nc.vector.tensor_copy)
+
+        def tok_quant(n):
+            cols = slice(512 * n, 512 * (n + 1))
+            nc.vector.quantize_mx(out=t1_codes[:, cols].bitcast(E5), scales=t1_scales[:, cols], in_=tok[:, cols, :].rearrange("p d j -> p (d j)"))
+
+        tags = (("w", 2), ("g", 3), ("dz", 1), ("acc", 2), ("g", 3), ("w", 2), ("acc", 2), ("g", 3))
+
+        def dw(n, engines):
+            for q in range(2):
+                st = work.tile([P, 4, 512], F32, name="wraw", tag="wraw", bufs=3, align_bytes=64)
+                for b in range(4):
+                    d = 4 * q + b
+                    tag, bufs = tags[d]
+                    ps = psum.tile([P, 512], F32, name="dwp", tag=tag, bufs=bufs)
+                    nc.tensor.matmul_mx(out=ps[:], lhsT=pv_codes[:, P * d : P * (d + 1)].bitcast(E4), lhsT_scale=pv_scales[:, P * d : P * (d + 1)], rhs=t1_codes[:, 512 * n : 512 * (n + 1)].bitcast(E5), rhs_scale=t1_scales[:, 512 * n : 512 * (n + 1)], start=True, stop=True)
+                    engines[d](st[:, b, :], ps[:])
+                    nc.sync.dma_start(out=out_1[P * d : P * (d + 1), 512 * n : 512 * (n + 1)], in_=st[:, b, :])
+
+        tok_quant(0)
+        dz1_quant(3, grp3)
+        dw(0, (v_neg, v_neg, s_neg, v_neg, s_neg, v_neg, s_neg, s_neg))
+        tok_quant(1)
+        dx(3, (v_neg, s_neg))
+        dw(1, (v_neg, s_neg, v_neg, s_neg, v_neg, s_neg, v_neg, s_neg))

@@ -19,8 +19,8 @@ ACT = mybir.ActivationFunctionType
 
 P = 128
 J = 256
+SPLIT = 224
 NCH = B * E // (P * J)
-ORDER = (1, 0, 3, 2)
 
 
 def tile_hebbianlayer_pb_v_kernel(tc, prev_act, W1, b1, W2, b2, dopamine, serotonin, glutamate, gaba, z1, h, grad_out, out_0, out_1):
@@ -28,7 +28,7 @@ def tile_hebbianlayer_pb_v_kernel(tc, prev_act, W1, b1, W2, b2, dopamine, seroto
     prev_v = prev_act.rearrange("(p j) d -> p j d", j=4)
     h_v = h.rearrange("(p j) k -> p j k", j=4)
     z1_v = z1.rearrange("(p j) d -> p j d", j=4)
-    g_v = grad_out.rearrange("(c p j) e -> p c j e", c=4, j=4)
+    g_v = grad_out.rearrange("(a e p j) u -> p a e j u", a=2, e=2, j=4)
     w2_v = W2.rearrange("(n b r) k -> r n b k", n=2, b=4)
     w1_v = W1.rearrange("(n b r) k -> r n b k", n=2, b=4)
     o0_v = out_0.rearrange("(p j) d -> p j d", j=4)
@@ -39,12 +39,10 @@ def tile_hebbianlayer_pb_v_kernel(tc, prev_act, W1, b1, W2, b2, dopamine, seroto
         psum = ctx.enter_context(tc.psum_pool(name="psum", bufs=2))
         ctx.enter_context(tc.manual_schedule())
 
-        ident_b = keep.tile([P, P], BF16, name="ident_b")
         ident_f = keep.tile([P, P], F32, name="ident_f")
         eps = keep.tile([P, 1], F32, name="eps")
         warm = keep.tile([P, 1], F32, name="warm")
         nc.vector.memset(eps[:], 1e-25)
-        make_identity(nc, ident_b[:])
         make_identity(nc, ident_f[:])
         nc.scalar.activation(warm[:], eps[:], ACT.Abs_reciprocal_sqrt)
 
@@ -59,8 +57,8 @@ def tile_hebbianlayer_pb_v_kernel(tc, prev_act, W1, b1, W2, b2, dopamine, seroto
         t1_scales = keep.tile([P, D], U8, name="t1_scales", align_bytes=64)
 
         hs, gs, ws, z1s = {}, {}, {}, {}
-        h2s, invs, inv2s, gps, xs, ys, ss, ts, os_ = {}, {}, {}, {}, {}, {}, {}, {}, {}
-        wg, dzg, dz2c, dz2s, acc, d1c = {}, {}, {}, {}, {}, {}
+        h2s, invs, inv2s, xs, ys, ss, ts, os_ = {}, {}, {}, {}, {}, {}, {}, {}
+        wg, dzg, dzx, dz2c, dz2s, acc, d1c, d1x, d1g = {}, {}, {}, {}, {}, {}, {}, {}, {}
 
         def load_h(i):
             if i < NCH:
@@ -70,7 +68,9 @@ def tile_hebbianlayer_pb_v_kernel(tc, prev_act, W1, b1, W2, b2, dopamine, seroto
         def load_g(k):
             if k < NCH // 2:
                 gs[k] = work.tile([P, 4, 2 * J], BF16, name="g", tag="g", bufs=2, align_bytes=64)
-                nc.sync.dma_start(out=gs[k][:], in_=g_v[:, :, k // 2, (k % 2) * 2 * J : (k % 2 + 1) * 2 * J])
+                planes = gs[k][:].rearrange("p (a e) u -> p a e u", e=2)
+                for e in range(2):
+                    nc.sync.dma_start(out=planes[:, :, 1 - e, :], in_=g_v[:, :, e, k // 2, (k % 2) * 2 * J : (k % 2 + 1) * 2 * J])
 
         def load_w(k):
             if k < 10:
@@ -83,7 +83,7 @@ def tile_hebbianlayer_pb_v_kernel(tc, prev_act, W1, b1, W2, b2, dopamine, seroto
             nc.sync.dma_start(out=z1s[t][:], in_=z1_v[:, t, :])
 
         def w_transposes(k, gg, half):
-            xt = psum.tile([P, 2, 2, P], F32, name="xt", tag="w", bufs=2)
+            xt = psum.tile([P, 2, 2, P], F32, name="xt", tag="w", bufs=3)
             words = ws[k][:].bitcast(F32)
             for bb in range(2):
                 for u in range(2):
@@ -92,7 +92,7 @@ def tile_hebbianlayer_pb_v_kernel(tc, prev_act, W1, b1, W2, b2, dopamine, seroto
 
         def w_copy(k, gg, half, xt):
             if half == 0:
-                wg[k, gg] = work.tile([P, 4, P, 4], BF16, name="wg", tag="wg", bufs=3, align_bytes=64)
+                wg[k, gg] = work.tile([P, 4, P, 4], BF16, name="wg", tag="wg", bufs=4, align_bytes=64)
             dst = wg[k, gg][:].bitcast(F32)
             nc.scalar.copy(dst[:, 2 * half : 2 * half + 2, :, :], xt[:].rearrange("p b u r -> p b r u"))
 
@@ -117,14 +117,12 @@ def tile_hebbianlayer_pb_v_kernel(tc, prev_act, W1, b1, W2, b2, dopamine, seroto
             inv2s[i] = work.tile([P, J], F32, name="inv2", tag="inv2", bufs=3, align_bytes=64)
             nc.scalar.activation(inv2s[i][:], invs[i][:], ACT.Square)
 
-        def pe_g(i):
-            gps[i] = psum.tile([P, 4, J], BF16, name="gp", tag="g", bufs=3)
-            for pos in range(4):
-                nc.tensor.matmul(gps[i][:, pos, :], lhsT=ident_b[:], rhs=gs[i // 2][:, ORDER[pos], (i % 2) * J : (i % 2 + 1) * J], start=True, stop=True)
+        def g_part(i):
+            return gs[i // 2][:, :, (i % 2) * J : (i % 2 + 1) * J]
 
         def v_x(i):
             xs[i] = work.tile([P, 4, J], F32, name="x", tag="x", bufs=3, align_bytes=64)
-            nc.vector.scalar_tensor_tensor(out=xs[i][:, 1:4, :], in0=invs[i][:].unsqueeze(1).to_broadcast([P, 3, J]), scalar=1e6, in1=gps[i][:, 1:4, :], op0=ALU.min, op1=ALU.mult)
+            nc.vector.scalar_tensor_tensor(out=xs[i][:, 1:4, :], in0=invs[i][:].unsqueeze(1).to_broadcast([P, 3, J]), scalar=1e6, in1=g_part(i)[:, 1:4, :], op0=ALU.min, op1=ALU.mult)
 
         def v_m(i):
             nc.vector.scalar_tensor_tensor(out=xs[i][:, 0, :], in0=invs[i][:], scalar=1e6, in1=inv2s[i][:], op0=ALU.is_lt, op1=ALU.mult)
@@ -136,18 +134,24 @@ def tile_hebbianlayer_pb_v_kernel(tc, prev_act, W1, b1, W2, b2, dopamine, seroto
             ys[i] = work.tile([P, 4, J], F32, name="y", tag="y", bufs=2, align_bytes=64)
             nc.vector.tensor_tensor(out=ys[i][:].rearrange("p (a e) j -> p a j e", e=2), in0=hs[i][:].rearrange("p j (a e) -> p a j e", e=2), in1=x_pairs(i), op=ALU.mult)
 
-        def g_s(i):
-            s1 = work.tile([P, J], F32, name="s1", tag="s1", bufs=2, align_bytes=64)
-            ss[i] = work.tile([P, J], F32, name="s", tag="s", bufs=2, align_bytes=64)
-            nc.gpsimd.tensor_tensor(out=s1[:], in0=ys[i][:, 0, :], in1=ys[i][:, 2, :], op=ALU.add)
-            nc.gpsimd.tensor_tensor(out=ss[i][:], in0=s1[:], in1=ys[i][:, 3, :], op=ALU.add)
+        def pe_s(i):
+            ss[i] = psum.tile([P, J], F32, name="s", tag="s", bufs=2)
+            for c in (0, 2, 3):
+                nc.tensor.matmul(ss[i][:], lhsT=ident_f[:], rhs=ys[i][:, c, :], start=(c == 0), stop=(c == 3))
+
+        def v_s1(i):
+            ss[i] = work.tile([P, J], F32, name="s1", tag="s1", bufs=1, align_bytes=64)
+            nc.vector.tensor_tensor(out=ss[i][:], in0=ys[i][:, 0, :], in1=ys[i][:, 2, :], op=ALU.add)
+
+        def v_s2(i):
+            nc.vector.tensor_tensor(out=ss[i][:], in0=ss[i][:], in1=ys[i][:, 3, :], op=ALU.add)
 
         def v_t(i):
             ts[i] = work.tile([P, J], F32, name="t", tag="t", bufs=2, align_bytes=64)
             nc.vector.tensor_tensor(out=ts[i][:], in0=ys[i][:, 1, :], in1=ss[i][:], op=ALU.mult)
 
         def v_d1(i):
-            nc.vector.tensor_tensor(out=xs[i][:, 0, :], in0=gps[i][:, 0, :], in1=ts[i][:], op=ALU.subtract)
+            nc.vector.tensor_tensor(out=xs[i][:, 0, :], in0=g_part(i)[:, 0, :], in1=ts[i][:], op=ALU.subtract)
 
         def v_o(i):
             os_[i] = work.tile([P, 2, J, 2], BF16, name="o", tag="o", bufs=3, align_bytes=64)
@@ -156,14 +160,37 @@ def tile_hebbianlayer_pb_v_kernel(tc, prev_act, W1, b1, W2, b2, dopamine, seroto
             for a in range(2):
                 nc.vector.scalar_tensor_tensor(out=os_[i][:, a, :, :], in0=h2p[:, a, :, :], scalar=1.0, in1=xp[:, a, :, :], op0=ALU.subtract, op1=ALU.mult)
 
+        def v_o_half(i, gg):
+            if gg == 0:
+                os_[i] = work.tile([P, 2, J, 2], BF16, name="o", tag="o", bufs=3, align_bytes=64)
+            cols = slice(P * gg, P * (gg + 1))
+            h2p = h2s[i][:].rearrange("p j (a e) -> p a j e", e=2)
+            xp = x_pairs(i)
+            for a in range(2):
+                nc.vector.scalar_tensor_tensor(out=os_[i][:, a, cols, :], in0=h2p[:, a, cols, :], scalar=1.0, in1=xp[:, a, cols, :], op0=ALU.subtract, op1=ALU.mult)
+
+        def dz_half(i, gg):
+            xt = psum.tile([P, 2, P], F32, name="dzh", tag="w", bufs=3)
+            words = os_[i][:].rearrange("p a j e -> p (a j e)").bitcast(F32)
+            for a in range(2):
+                nc.tensor.transpose(xt[:, a, :], words[:, a * J + gg * P : a * J + (gg + 1) * P], ident_f[:])
+            return xt
+
+        def dz_quant_half(i, gg):
+            t, g = i // 4, 2 * (i % 4) + gg
+            nc.vector.quantize_mx(out=dz2c[t][:, g, :].bitcast(E5), scales=dz2s[t][:, g, :], in_=dzg[i][:, gg, :, :].rearrange("p r t -> p (r t)"))
+
         def dz_transposes(i):
             xt = psum.tile([P, 2, 2, P], F32, name="dzt", tag="dz", bufs=1)
             words = os_[i][:].rearrange("p a j e -> p (a j e)").bitcast(F32)
             for gg in range(2):
                 for a in range(2):
                     nc.tensor.transpose(xt[:, gg, a, :], words[:, a * J + gg * P : a * J + (gg + 1) * P], ident_f[:])
+            dzx[i] = xt
+
+        def dz_copy(i):
             dzg[i] = work.tile([P, 2, P, 4], BF16, name="dzg", tag="dzg", bufs=2, align_bytes=64)
-            nc.scalar.copy(dzg[i][:].bitcast(F32), xt[:].rearrange("p g a r -> p g r a"))
+            nc.scalar.copy(dzg[i][:].bitcast(F32), dzx[i][:].rearrange("p g a r -> p g r a"))
 
         def dz_quant(i):
             t, u = i // 4, i % 4
@@ -184,20 +211,21 @@ def tile_hebbianlayer_pb_v_kernel(tc, prev_act, W1, b1, W2, b2, dopamine, seroto
         def v_mask(t, n):
             nc.vector.scalar_tensor_tensor(out=dz1[:, t, 512 * n : 512 * (n + 1)], in0=z1s[t][:, 512 * n : 512 * (n + 1)], scalar=0.0, in1=acc[t, n][:], op0=ALU.is_gt, op1=ALU.mult)
 
-        def dz1_transposes(t, copy):
-            xt = psum.tile([P, 2, 2, P], F32, name="d1t", tag="w", bufs=2)
+        def dz1_transposes(t):
+            d1x[t] = psum.tile([P, 2, 2, P], F32, name="d1t", tag="w", bufs=3)
             words = dz1[:, t, :].bitcast(F32)
             for g in range(2):
                 for u in range(2):
-                    nc.tensor.transpose(xt[:, g, u, :], words[:, 256 * g + u : 256 * (g + 1) : 2], ident_f[:])
-            grp = work.tile([P, 2, P, 4], BF16, name="d1g", tag="d1g", bufs=2, align_bytes=64)
-            copy(grp[:].bitcast(F32), xt[:].rearrange("p g u r -> p g r u"))
-            return grp
+                    nc.tensor.transpose(d1x[t][:, g, u, :], words[:, 256 * g + u : 256 * (g + 1) : 2], ident_f[:])
 
-        def dz1_quant(t, grp):
+        def dz1_copy(t, copy):
+            d1g[t] = work.tile([P, 2, P, 4], BF16, name="d1g", tag="d1g", bufs=2, align_bytes=64)
+            copy(d1g[t][:].bitcast(F32), d1x[t][:].rearrange("p g u r -> p g r u"))
+
+        def dz1_quant(t):
             co = work.tile([P, 2, P], U32, name="d1c", tag="d1c", bufs=2, align_bytes=64)
             sc = work.tile([P, 2, P], U8, name="d1s", tag="d1s", bufs=2, align_bytes=64)
-            nc.vector.quantize_mx(out=co[:].rearrange("p g r -> p (g r)").bitcast(E5), scales=sc[:].rearrange("p g r -> p (g r)"), in_=grp[:].rearrange("p g r t -> p (g r t)"))
+            nc.vector.quantize_mx(out=co[:].rearrange("p g r -> p (g r)").bitcast(E5), scales=sc[:].rearrange("p g r -> p (g r)"), in_=d1g[t][:].rearrange("p g r t -> p (g r t)"))
             d1c[t] = (co, sc)
 
         def s_neg(dst, src):
@@ -210,7 +238,7 @@ def tile_hebbianlayer_pb_v_kernel(tc, prev_act, W1, b1, W2, b2, dopamine, seroto
             co, sc = d1c[t]
             ost = work.tile([P, D], F32, name="ost", tag="ost", bufs=2, align_bytes=64)
             for n in range(2):
-                ps = psum.tile([P, 512], F32, name="dxp", tag="w", bufs=2)
+                ps = psum.tile([P, 512], F32, name="dxp", tag="w", bufs=3)
                 for g in range(2):
                     nc.tensor.matmul_mx(out=ps[:], lhsT=co[:, g, :].bitcast(E5), lhsT_scale=sc[:, g, :], rhs=w1_codes[n][:, g, :].bitcast(E4), rhs_scale=w1_scales[n][:, g, :], start=(g == 0), stop=(g == 1))
                 engines[n](ost[:, 512 * n : 512 * (n + 1)], ps[:])
@@ -232,7 +260,7 @@ def tile_hebbianlayer_pb_v_kernel(tc, prev_act, W1, b1, W2, b2, dopamine, seroto
         for k in range(2):
             cols = slice(512 * k, 512 * (k + 1))
             nc.vector.tensor_copy(out=pvg[:, cols, :], in_=pv[:, :, cols].rearrange("p j d -> p d j"))
-        for k in range(2):
+        def pv_quant(k):
             cols = slice(512 * k, 512 * (k + 1))
             nc.vector.quantize_mx(out=pv_codes[:, cols].bitcast(E4), scales=pv_scales[:, cols], in_=pvg[:, cols, :].rearrange("p d j -> p (d j)"))
 
@@ -240,11 +268,13 @@ def tile_hebbianlayer_pb_v_kernel(tc, prev_act, W1, b1, W2, b2, dopamine, seroto
             sc_square(i)
             sc_inv(i)
             sc_inv2(i)
-            pe_g(i)
+        pv_quant(0)
         v_x(0)
         v_m(0)
+        pv_quant(1)
 
         for i in range(NCH):
+            last = i == NCH - 1
             load_w(i + 2)
             load_h(i + 4)
             if i % 2 == 0:
@@ -252,52 +282,57 @@ def tile_hebbianlayer_pb_v_kernel(tc, prev_act, W1, b1, W2, b2, dopamine, seroto
             if i in (5, 6, 10, 12):
                 load_z1({5: 0, 6: 1, 10: 2, 12: 3}[i])
 
-            if i >= 2:
-                dz_transposes(i - 2)
             v_y(i)
-            g_s(i)
+            if i >= 1:
+                v_t(i - 1)
+            if i < 10:
+                w_copy(i, 0, 0, w_transposes(i, 0, 0))
             if i + 2 < NCH:
                 sc_square(i + 2)
             if i < 10:
-                xa = w_transposes(i, 0, 0)
-                w_copy(i, 0, 0, xa)
+                w_copy(i, 0, 1, w_transposes(i, 0, 1))
             if i + 2 < NCH:
                 sc_inv(i + 2)
             if i < 10:
-                xa = w_transposes(i, 0, 1)
-                w_copy(i, 0, 1, xa)
+                w_copy(i, 1, 0, w_transposes(i, 1, 0))
             if i + 2 < NCH:
                 sc_inv2(i + 2)
-            if i + 1 < NCH:
+            if last:
+                v_s1(i)
+            else:
                 v_x(i + 1)
             if i >= 1:
                 v_d1(i - 1)
-            if i + 2 < NCH:
-                pe_g(i + 2)
-            if i < 10:
-                for half in range(2):
-                    xa = w_transposes(i, 1, half)
-                    w_copy(i, 1, half, xa)
-            if i + 1 < NCH:
+            if last:
+                v_s2(i)
+            else:
                 v_m(i + 1)
-            w_quant(i - 1, 1)
+                pe_s(i)
             if i >= 1:
                 v_o(i - 1)
+            if last:
+                v_t(i)
+            w_quant(i - 1, 0)
+            w_quant(i - 1, 1)
             if i >= 2:
                 dz_quant(i - 2)
-            if i == 9:
-                v_mask(0, 0)
-                v_mask(0, 1)
-            if i == 10:
-                v_mask(1, 0)
-                v_mask(1, 1)
-            if i == 14:
-                v_mask(2, 0)
-                v_mask(2, 1)
-            w_quant(i, 0)
-            v_t(i)
+            if i in (9, 10, 14):
+                t = {9: 0, 10: 1, 14: 2}[i]
+                v_mask(t, 0)
+                v_mask(t, 1)
+            if i in (10, 11, 15):
+                dz1_quant({10: 0, 11: 1, 15: 2}[i])
 
-            if i == 8 or i == 9 or i == 13:
+            if i < 10:
+                w_copy(i, 1, 1, w_transposes(i, 1, 1))
+            if i >= 1:
+                dz_transposes(i - 1)
+                dz_copy(i - 1)
+            if i in (9, 10, 14):
+                t = {9: 0, 10: 1, 14: 2}[i]
+                dz1_transposes(t)
+                dz1_copy(t, nc.scalar.copy)
+            if i in (8, 9, 13):
                 t = {8: 0, 9: 1, 13: 2}[i]
                 for n in range(2):
                     for g in range(8):
@@ -306,51 +341,60 @@ def tile_hebbianlayer_pb_v_kernel(tc, prev_act, W1, b1, W2, b2, dopamine, seroto
                 for g in (2 * (i - 14), 2 * (i - 14) + 1):
                     for n in range(2):
                         mm_dhid(3, n, g)
-            if i in (11, 12, 15):
-                t = {11: 0, 12: 1, 15: 2}[i]
-                grp = dz1_transposes(t, nc.scalar.copy)
-                dz1_quant(t, grp)
-                dx(t, (s_neg, s_neg))
+            if i in (10, 11):
+                dx({10: 0, 11: 1}[i], (s_neg, s_neg))
 
-        dz_transposes(NCH - 2)
-        v_d1(NCH - 1)
-        dz_quant(NCH - 2)
-        v_o(NCH - 1)
+        z = NCH - 1
+        v_d1(z)
+        dz_quant(z - 1)
         for g in (4, 5):
             for n in range(2):
                 mm_dhid(3, n, g)
-        dz_transposes(NCH - 1)
-        dz_quant(NCH - 1)
-        for n in range(2):
-            for g in (6, 7):
-                mm_dhid(3, n, g)
-        v_mask(3, 0)
-        v_mask(3, 1)
+        halves = []
+        for gg in range(2):
+            v_o_half(z, gg)
+            halves.append(dz_half(z, gg))
+        dzg[z] = work.tile([P, 2, P, 4], BF16, name="dzg", tag="dzg", bufs=2, align_bytes=64)
+        for gg, copy in ((0, nc.scalar.copy), (1, nc.vector.tensor_copy)):
+            copy(dzg[z][:, gg, :, :].bitcast(F32), halves[gg][:].rearrange("p a r -> p r a"))
+        dx(2, (s_neg, s_neg))
+        for gg in range(2):
+            dz_quant_half(z, gg)
+            for n in range(2):
+                mm_dhid(3, n, 6 + gg)
         tok = work.tile([P, D, 4], BF16, name="tok", tag="tok", bufs=1, align_bytes=64)
-        nc.vector.tensor_copy(out=tok[:, 0:512, :], in_=dz1[:, :, 0:512].rearrange("p j d -> p d j"))
-        nc.scalar.copy(tok[:, 512:1024, :], dz1[:, :, 512:1024].rearrange("p j d -> p d j"))
-        grp3 = dz1_transposes(3, nc.vector.tensor_copy)
+
+        def tok_copy(copy, lo, hi):
+            copy(tok[:, lo:hi, :], dz1[:, :, lo:hi].rearrange("p j d -> p d j"))
+
+        v_mask(3, 0)
+        tok_copy(nc.scalar.copy, 0, SPLIT)
+        tok_copy(nc.vector.tensor_copy, SPLIT, 512)
 
         def tok_quant(n):
             cols = slice(512 * n, 512 * (n + 1))
             nc.vector.quantize_mx(out=t1_codes[:, cols].bitcast(E5), scales=t1_scales[:, cols], in_=tok[:, cols, :].rearrange("p d j -> p (d j)"))
 
-        tags = (("w", 2), ("g", 3), ("dz", 1), ("acc", 2), ("g", 3), ("w", 2), ("acc", 2), ("g", 3))
+        tags = (("w", 3), ("s", 2), ("dz", 1), ("w", 3), ("s", 2), ("w", 3), ("dz", 1), ("acc", 2))
 
-        def dw(n, engines):
-            for q in range(2):
-                st = work.tile([P, 4, 512], F32, name="wraw", tag="wraw", bufs=3, align_bytes=64)
-                for b in range(4):
-                    d = 4 * q + b
-                    tag, bufs = tags[d]
-                    ps = psum.tile([P, 512], F32, name="dwp", tag=tag, bufs=bufs)
+        def dw(n, engines, tag, bufs):
+            for q in range(4):
+                st = work.tile([P, 2, 512], F32, name="st", tag=tag, bufs=bufs, align_bytes=64)
+                for b in range(2):
+                    d = 2 * q + b
+                    pt, pb = tags[d]
+                    ps = psum.tile([P, 512], F32, name="dwp", tag=pt, bufs=pb)
                     nc.tensor.matmul_mx(out=ps[:], lhsT=pv_codes[:, P * d : P * (d + 1)].bitcast(E4), lhsT_scale=pv_scales[:, P * d : P * (d + 1)], rhs=t1_codes[:, 512 * n : 512 * (n + 1)].bitcast(E5), rhs_scale=t1_scales[:, 512 * n : 512 * (n + 1)], start=True, stop=True)
                     engines[d](st[:, b, :], ps[:])
                     nc.sync.dma_start(out=out_1[P * d : P * (d + 1), 512 * n : 512 * (n + 1)], in_=st[:, b, :])
 
         tok_quant(0)
-        dz1_quant(3, grp3)
-        dw(0, (v_neg, v_neg, s_neg, v_neg, s_neg, v_neg, s_neg, s_neg))
+        v_mask(3, 1)
+        tok_copy(nc.vector.tensor_copy, 512, 1024)
+        dz1_transposes(3)
         tok_quant(1)
+        dz1_copy(3, nc.vector.tensor_copy)
+        dw(0, (s_neg, s_neg, s_neg, s_neg, s_neg, v_neg, s_neg, v_neg), "h", 5)
+        dz1_quant(3)
+        dw(1, (v_neg, s_neg, v_neg, s_neg, v_neg, s_neg, v_neg, s_neg), "wg", 4)
         dx(3, (v_neg, s_neg))
-        dw(1, (v_neg, s_neg, v_neg, s_neg, v_neg, s_neg, v_neg, s_neg))

@@ -18,8 +18,9 @@ ALU = mybir.AluOpType
 ACT = mybir.ActivationFunctionType
 
 P = 128
+PRM = {'w_at': {1: [0], 2: [1], 3: [2], 4: [3], 5: [4], 6: [5], 7: [6], 8: [7], 9: [8], 10: [9]}, 'wload': {2: [2], 3: [3], 4: [4], 5: [5], 6: [6], 7: [7], 8: [8], 9: [9]}, 'wfirst': True, 'gstep': 1, 'z1': [5, 8, 10, 14], 'mxa': {3: [(0, 0, 0, 2)], 4: [(0, 0, 2, 4)], 5: [(0, 0, 4, 6)], 6: [(0, 0, 6, 8)], 7: [(0, 1, 0, 2)], 9: [(0, 1, 2, 4), (0, 1, 4, 6), (1, 0, 0, 2)], 10: [(0, 1, 6, 8), (1, 0, 2, 4), (1, 0, 4, 6)], 11: [(1, 0, 6, 8), (1, 1, 0, 2)], 12: [(1, 1, 2, 4), (1, 1, 4, 6), (1, 1, 6, 8), (2, 0, 0, 2), (2, 0, 2, 4)], 13: [(2, 1, 0, 2), (2, 1, 2, 4)], 14: [(2, 0, 4, 6), (2, 1, 4, 6)], 15: [(2, 0, 6, 8), (2, 1, 6, 8), (3, 0, 0, 2), (3, 1, 0, 2)]}, 'mxc': {}, 'mask': {8: [(0, 0)], 10: [(0, 1)], 11: [(1, 0)], 12: [(1, 1)], 15: [(2, 0), (2, 1)]}, 'tr': {11: 0, 14: 1}, 'q': {11: 0, 14: 1}, 'dx': {13: 0, 15: 1}, 'trt': [2], 'qt': [2], 'dxt': [2], 'pesum': [1, 2, 3, 4, 5, 6, 7, 8, 9, 10, 11, 12, 13, 14], 'mxt': [[(3, 0, 2, 4), (3, 1, 2, 4)], [(3, 0, 4, 6), (3, 1, 4, 6)]]}
 J = 256
-SPLIT = 224
+SPLIT = 192
 NCH = B * E // (P * J)
 
 
@@ -65,12 +66,14 @@ def tile_hebbianlayer_pb_v_kernel(tc, prev_act, W1, b1, W2, b2, dopamine, seroto
                 hs[i] = work.tile([P, J, 4], F32, name="h", tag="h", bufs=5, align_bytes=64)
                 nc.sync.dma_start(out=hs[i][:].rearrange("p j c -> p (j c)"), in_=h_v[:, i // 4, (i % 4) * 4 * J : (i % 4 + 1) * 4 * J])
 
-        def load_g(k):
-            if k < NCH // 2:
-                gs[k] = work.tile([P, 4, 2 * J], BF16, name="g", tag="g", bufs=2, align_bytes=64)
-                planes = gs[k][:].rearrange("p (a e) u -> p a e u", e=2)
-                for e in range(2):
-                    nc.sync.dma_start(out=planes[:, :, 1 - e, :], in_=g_v[:, :, e, k // 2, (k % 2) * 2 * J : (k % 2 + 1) * 2 * J])
+        def load_g(t, lo=0, hi=E):
+            if t > 3:
+                return
+            if lo == 0:
+                gs[t] = work.tile([P, 4, E], BF16, name="g", tag="g", bufs=2, align_bytes=64)
+            planes = gs[t][:].rearrange("p (r a) u -> p r a u", r=2)
+            for e in range(2):
+                nc.sync.dma_start(out=planes[:, 1 - e, :, lo:hi], in_=g_v[:, :, e, t, lo:hi])
 
         def load_w(k):
             if k < 10:
@@ -91,34 +94,32 @@ def tile_hebbianlayer_pb_v_kernel(tc, prev_act, W1, b1, W2, b2, dopamine, seroto
             return xt
 
         def w_copy(k, gg, half, xt):
-            if half == 0:
-                wg[k, gg] = work.tile([P, 4, P, 4], BF16, name="wg", tag="wg", bufs=4, align_bytes=64)
-            dst = wg[k, gg][:].bitcast(F32)
-            nc.scalar.copy(dst[:, 2 * half : 2 * half + 2, :, :], xt[:].rearrange("p b u r -> p b r u"))
+            if gg == 0 and half == 0:
+                wg[k] = work.tile([P, 2, 4, P, 4], BF16, name="wg", tag="wg", bufs=2, align_bytes=64)
+            dst = wg[k][:].bitcast(F32)
+            nc.scalar.copy(dst[:, gg, 2 * half : 2 * half + 2, :, :], xt[:].rearrange("p b u r -> p b r u"))
 
-        def w_quant(k, gg):
-            if k < 0 or k > 9:
-                return
+        def w_quant(k):
             if k < 8:
-                g, co, sc = 2 * (k % 4) + gg, w2_codes[k // 4], w2_scales[k // 4]
+                g, co, sc = 2 * (k % 4), w2_codes[k // 4], w2_scales[k // 4]
             else:
-                g, co, sc = gg, w1_codes[k - 8], w1_scales[k - 8]
-            nc.vector.quantize_mx(out=co[:, g, :].bitcast(E4), scales=sc[:, g, :], in_=wg[k, gg][:].rearrange("p b r t -> p (b r t)"))
+                g, co, sc = 0, w1_codes[k - 8], w1_scales[k - 8]
+            nc.vector.quantize_mx(out=co[:, g : g + 2, :].rearrange("p g n -> p (g n)").bitcast(E4), scales=sc[:, g : g + 2, :].rearrange("p g n -> p (g n)"), in_=wg[k][:].rearrange("p g b r t -> p (g b r t)"))
 
         def sc_square(i):
-            h2s[i] = work.tile([P, J, 4], F32, name="h2", tag="h2", bufs=4, align_bytes=64)
-            nc.scalar.activation(h2s[i][:].rearrange("p j c -> p (j c)"), hs[i][:].rearrange("p j c -> p (j c)"), ACT.Square)
+            h2s[i] = work.tile([P, 2, J, 2], F32, name="h2", tag="h2", bufs=4, align_bytes=64)
+            nc.scalar.activation(h2s[i][:].rearrange("p a j e -> p j a e"), hs[i][:].rearrange("p j (a e) -> p j a e", e=2), ACT.Square)
 
-        def sc_inv(i):
-            invs[i] = work.tile([P, J], F32, name="inv", tag="inv", bufs=3, align_bytes=64)
-            nc.scalar.activation(invs[i][:], h2s[i][:, :, 1], ACT.Abs_reciprocal_sqrt, bias=eps[:])
+        def sc_inv(i, src=None):
+            invs[i] = work.tile([P, J], F32, name="inv", tag="inv", bufs=2, align_bytes=64)
+            nc.scalar.activation(invs[i][:], h2s[i][:, 0, :, 1] if src is None else src, ACT.Abs_reciprocal_sqrt, bias=eps[:])
 
         def sc_inv2(i):
-            inv2s[i] = work.tile([P, J], F32, name="inv2", tag="inv2", bufs=3, align_bytes=64)
+            inv2s[i] = work.tile([P, J], F32, name="inv2", tag="inv2", bufs=2, align_bytes=64)
             nc.scalar.activation(inv2s[i][:], invs[i][:], ACT.Square)
 
         def g_part(i):
-            return gs[i // 2][:, :, (i % 2) * J : (i % 2 + 1) * J]
+            return gs[i // 4][:, :, (i % 4) * J : (i % 4 + 1) * J]
 
         def v_x(i):
             xs[i] = work.tile([P, 4, J], F32, name="x", tag="x", bufs=3, align_bytes=64)
@@ -128,7 +129,7 @@ def tile_hebbianlayer_pb_v_kernel(tc, prev_act, W1, b1, W2, b2, dopamine, seroto
             nc.vector.scalar_tensor_tensor(out=xs[i][:, 0, :], in0=invs[i][:], scalar=1e6, in1=inv2s[i][:], op0=ALU.is_lt, op1=ALU.mult)
 
         def x_pairs(i):
-            return xs[i][:].rearrange("p (a e) j -> p a j e", e=2)[:, :, :, ::-1]
+            return xs[i][:].rearrange("p (r a) j -> p a j r", r=2)[:, :, :, ::-1]
 
         def v_y(i):
             ys[i] = work.tile([P, 4, J], F32, name="y", tag="y", bufs=2, align_bytes=64)
@@ -136,8 +137,10 @@ def tile_hebbianlayer_pb_v_kernel(tc, prev_act, W1, b1, W2, b2, dopamine, seroto
 
         def pe_s(i):
             ss[i] = psum.tile([P, J], F32, name="s", tag="s", bufs=2)
-            for c in (0, 2, 3):
-                nc.tensor.matmul(ss[i][:], lhsT=ident_f[:], rhs=ys[i][:, c, :], start=(c == 0), stop=(c == 3))
+            pe_s_part(i, 0)
+
+        def pe_s_part(i, c):
+            nc.tensor.matmul(ss[i][:], lhsT=ident_f[:], rhs=ys[i][:, c, :], start=(c == 0), stop=(c == 3))
 
         def v_s1(i):
             ss[i] = work.tile([P, J], F32, name="s1", tag="s1", bufs=1, align_bytes=64)
@@ -154,20 +157,17 @@ def tile_hebbianlayer_pb_v_kernel(tc, prev_act, W1, b1, W2, b2, dopamine, seroto
             nc.vector.tensor_tensor(out=xs[i][:, 0, :], in0=g_part(i)[:, 0, :], in1=ts[i][:], op=ALU.subtract)
 
         def v_o(i):
-            os_[i] = work.tile([P, 2, J, 2], BF16, name="o", tag="o", bufs=3, align_bytes=64)
-            h2p = h2s[i][:].rearrange("p j (a e) -> p a j e", e=2)
-            xp = x_pairs(i)
-            for a in range(2):
-                nc.vector.scalar_tensor_tensor(out=os_[i][:, a, :, :], in0=h2p[:, a, :, :], scalar=1.0, in1=xp[:, a, :, :], op0=ALU.subtract, op1=ALU.mult)
+            os_[i] = work.tile([P, 2, J, 2], BF16, name="o", tag="o", bufs=2, align_bytes=64)
+            xp = xs[i][:].rearrange("p (r a) j -> p (a j) r", r=2)[:, :, ::-1]
+            nc.vector.scalar_tensor_tensor(out=os_[i][:].rearrange("p a j e -> p (a j) e"), in0=h2s[i][:].rearrange("p a j e -> p (a j) e"), scalar=1.0, in1=xp, op0=ALU.subtract, op1=ALU.mult)
 
         def v_o_half(i, gg):
             if gg == 0:
-                os_[i] = work.tile([P, 2, J, 2], BF16, name="o", tag="o", bufs=3, align_bytes=64)
+                os_[i] = work.tile([P, 2, J, 2], BF16, name="o", tag="o", bufs=2, align_bytes=64)
             cols = slice(P * gg, P * (gg + 1))
-            h2p = h2s[i][:].rearrange("p j (a e) -> p a j e", e=2)
             xp = x_pairs(i)
             for a in range(2):
-                nc.vector.scalar_tensor_tensor(out=os_[i][:, a, cols, :], in0=h2p[:, a, cols, :], scalar=1.0, in1=xp[:, a, cols, :], op0=ALU.subtract, op1=ALU.mult)
+                nc.vector.scalar_tensor_tensor(out=os_[i][:, a, cols, :], in0=h2s[i][:, a, cols, :], scalar=1.0, in1=xp[:, a, cols, :], op0=ALU.subtract, op1=ALU.mult)
 
         def dz_half(i, gg):
             xt = psum.tile([P, 2, P], F32, name="dzh", tag="w", bufs=3)
@@ -205,7 +205,7 @@ def tile_hebbianlayer_pb_v_kernel(tc, prev_act, W1, b1, W2, b2, dopamine, seroto
 
         def mm_dhid(t, n, g):
             if g == 0:
-                acc[t, n] = psum.tile([P, 512], F32, name="acc", tag="acc", bufs=2)
+                acc[t, n] = psum.tile([P, 512], F32, name="acc", tag="w" if t == 3 else "acc", bufs=3 if t == 3 else 2)
             nc.tensor.matmul_mx(out=acc[t, n][:], lhsT=dz2c[t][:, g, :].bitcast(E5), lhsT_scale=dz2s[t][:, g, :], rhs=w2_codes[n][:, g, :].bitcast(E4), rhs_scale=w2_scales[n][:, g, :], start=(g == 0), stop=(g == 7))
 
         def v_mask(t, n):
@@ -219,7 +219,7 @@ def tile_hebbianlayer_pb_v_kernel(tc, prev_act, W1, b1, W2, b2, dopamine, seroto
                     nc.tensor.transpose(d1x[t][:, g, u, :], words[:, 256 * g + u : 256 * (g + 1) : 2], ident_f[:])
 
         def dz1_copy(t, copy):
-            d1g[t] = work.tile([P, 2, P, 4], BF16, name="d1g", tag="d1g", bufs=2, align_bytes=64)
+            d1g[t] = work.tile([P, 2, P, 4], BF16, name="d1g", tag="d1g", bufs=1, align_bytes=64)
             copy(d1g[t][:].bitcast(F32), d1x[t][:].rearrange("p g u r -> p g r u"))
 
         def dz1_quant(t):
@@ -245,119 +245,145 @@ def tile_hebbianlayer_pb_v_kernel(tc, prev_act, W1, b1, W2, b2, dopamine, seroto
             nc.sync.dma_start(out=o0_v[:, t, :], in_=ost[:])
 
         pv = work.tile([P, 4, 1024], BF16, name="wraw", tag="wraw", bufs=3, align_bytes=64)
-        for k in range(2):
+        def load_pv(k):
             nc.sync.dma_start(out=pv[:, :, 512 * k : 512 * (k + 1)], in_=prev_v[:, :, 512 * k : 512 * (k + 1)])
+
+        load_pv(0)
         load_h(0)
-        load_g(0)
+        load_g(0, 0, 512)
         load_h(1)
-        load_w(0)
+        load_pv(1)
         load_h(2)
-        load_g(1)
-        load_w(1)
+        load_w(0)
+        load_g(0, 512, 1024)
         load_h(3)
+        load_w(1)
 
         pvg = work.tile([P, D, 4], BF16, name="tok", tag="tok", bufs=1, align_bytes=64)
-        for k in range(2):
+
+        def pv_copy(k):
             cols = slice(512 * k, 512 * (k + 1))
             nc.vector.tensor_copy(out=pvg[:, cols, :], in_=pv[:, :, cols].rearrange("p j d -> p d j"))
+
         def pv_quant(k):
             cols = slice(512 * k, 512 * (k + 1))
             nc.vector.quantize_mx(out=pv_codes[:, cols].bitcast(E4), scales=pv_scales[:, cols], in_=pvg[:, cols, :].rearrange("p d j -> p (d j)"))
 
-        for i in range(2):
-            sc_square(i)
-            sc_inv(i)
-            sc_inv2(i)
+        pv_copy(0)
+        sq = keep.tile([P, J], F32, name="sq")
+        nc.scalar.activation(sq[:], hs[0][:, :, 1], ACT.Square)
+        sc_inv(0, sq[:])
+        sc_square(0)
+        sc_inv2(0)
+        sc_square(1)
+        sc_inv(1)
+        sc_inv2(1)
         pv_quant(0)
         v_x(0)
         v_m(0)
-        pv_quant(1)
 
+        def mx_list(lst):
+            for t, n, g0, g1 in lst:
+                for g in range(g0, g1):
+                    mm_dhid(t, n, g)
+
+        mx_a, mx_c, mask_at, t_at, q_at, dx_at, pe_sum = PRM['mxa'], PRM['mxc'], PRM['mask'], PRM['tr'], PRM['q'], PRM['dx'], PRM['pesum']
         for i in range(NCH):
             last = i == NCH - 1
-            load_w(i + 2)
+            pieces = PRM['w_at'].get(i, ())
+            units = [(k, gg, half) for k in pieces for gg in range(2) for half in range(2)]
+            cut1, cut2 = (2, 3) if len(units) == 4 else (3, 6)
+            for k in PRM['wload'].get(i, ()) if PRM['wfirst'] else ():
+                load_w(k)
             load_h(i + 4)
-            if i % 2 == 0:
-                load_g(i // 2 + 2)
-            if i in (5, 6, 10, 12):
-                load_z1({5: 0, 6: 1, 10: 2, 12: 3}[i])
+            for k in PRM['wload'].get(i, ()) if not PRM['wfirst'] else ():
+                load_w(k)
+            if i % 4 == PRM['gstep']:
+                load_g(i // 4 + 1)
+            if i in PRM['z1']:
+                load_z1(PRM['z1'].index(i))
 
-            v_y(i)
-            if i >= 1:
-                v_t(i - 1)
-            if i < 10:
-                w_copy(i, 0, 0, w_transposes(i, 0, 0))
             if i + 2 < NCH:
                 sc_square(i + 2)
-            if i < 10:
-                w_copy(i, 0, 1, w_transposes(i, 0, 1))
+            if i >= 2:
+                dz_transposes(i - 2)
+                dz_copy(i - 2)
             if i + 2 < NCH:
                 sc_inv(i + 2)
-            if i < 10:
-                w_copy(i, 1, 0, w_transposes(i, 1, 0))
+            v_y(i)
+            mx_list(mx_a.get(i, ()))
+            for k, gg, half in units[:1]:
+                w_copy(k, gg, half, w_transposes(k, gg, half))
             if i + 2 < NCH:
                 sc_inv2(i + 2)
-            if last:
-                v_s1(i)
-            else:
+            if i in t_at:
+                dz1_transposes(t_at[i])
+                dz1_copy(t_at[i], nc.scalar.copy)
+            for k, gg, half in units[1:cut1]:
+                w_copy(k, gg, half, w_transposes(k, gg, half))
+            if i in pe_sum:
+                pe_s(i)
+            for k, gg, half in units[cut1:cut2]:
+                w_copy(k, gg, half, w_transposes(k, gg, half))
+            if i in pe_sum:
+                pe_s_part(i, 2)
+            for k, gg, half in units[cut2:]:
+                w_copy(k, gg, half, w_transposes(k, gg, half))
+            if i in pe_sum:
+                pe_s_part(i, 3)
+            if i in dx_at:
+                dx(dx_at[i], (s_neg, s_neg))
+            if i == 0:
+                pv_copy(1)
+            if not last:
                 v_x(i + 1)
+            if i == 0:
+                pv_quant(1)
+            if i >= 1 and i - 1 in pe_sum:
+                v_t(i - 1)
+            if i not in pe_sum:
+                v_s1(i)
+            if not last:
+                v_m(i + 1)
             if i >= 1:
                 v_d1(i - 1)
-            if last:
+            for k in PRM['w_at'].get(i - 1, ()):
+                w_quant(k)
+            if i not in pe_sum:
                 v_s2(i)
-            else:
-                v_m(i + 1)
-                pe_s(i)
-            if i >= 1:
-                v_o(i - 1)
-            if last:
-                v_t(i)
-            w_quant(i - 1, 0)
-            w_quant(i - 1, 1)
             if i >= 2:
                 dz_quant(i - 2)
-            if i in (9, 10, 14):
-                t = {9: 0, 10: 1, 14: 2}[i]
-                v_mask(t, 0)
-                v_mask(t, 1)
-            if i in (10, 11, 15):
-                dz1_quant({10: 0, 11: 1, 15: 2}[i])
-
-            if i < 10:
-                w_copy(i, 1, 1, w_transposes(i, 1, 1))
             if i >= 1:
-                dz_transposes(i - 1)
-                dz_copy(i - 1)
-            if i in (9, 10, 14):
-                t = {9: 0, 10: 1, 14: 2}[i]
-                dz1_transposes(t)
-                dz1_copy(t, nc.scalar.copy)
-            if i in (8, 9, 13):
-                t = {8: 0, 9: 1, 13: 2}[i]
-                for n in range(2):
-                    for g in range(8):
-                        mm_dhid(t, n, g)
-            if i == 14 or i == 15:
-                for g in (2 * (i - 14), 2 * (i - 14) + 1):
-                    for n in range(2):
-                        mm_dhid(3, n, g)
-            if i in (10, 11):
-                dx({10: 0, 11: 1}[i], (s_neg, s_neg))
+                v_o(i - 1)
+            if i not in pe_sum:
+                v_t(i)
+            for t, n in mask_at.get(i, ()):
+                v_mask(t, n)
+            if i in q_at:
+                dz1_quant(q_at[i])
+            mx_list(mx_c.get(i, ()))
 
         z = NCH - 1
+        dz_transposes(z - 1)
+        dz_copy(z - 1)
         v_d1(z)
+        mx_list(PRM['mxt'][0])
+        for t in PRM['trt']:
+            dz1_transposes(t)
+            dz1_copy(t, nc.scalar.copy)
         dz_quant(z - 1)
-        for g in (4, 5):
-            for n in range(2):
-                mm_dhid(3, n, g)
-        halves = []
-        for gg in range(2):
-            v_o_half(z, gg)
-            halves.append(dz_half(z, gg))
+        mx_list(PRM['mxt'][1])
+        v_o_half(z, 0)
+        h0 = dz_half(z, 0)
+        v_o_half(z, 1)
+        h1 = dz_half(z, 1)
+        for t in PRM['qt']:
+            dz1_quant(t)
         dzg[z] = work.tile([P, 2, P, 4], BF16, name="dzg", tag="dzg", bufs=2, align_bytes=64)
-        for gg, copy in ((0, nc.scalar.copy), (1, nc.vector.tensor_copy)):
-            copy(dzg[z][:, gg, :, :].bitcast(F32), halves[gg][:].rearrange("p a r -> p r a"))
-        dx(2, (s_neg, s_neg))
+        nc.scalar.copy(dzg[z][:, 0, :, :].bitcast(F32), h0[:].rearrange("p a r -> p r a"))
+        nc.vector.tensor_copy(out=dzg[z][:, 1, :, :].bitcast(F32), in_=h1[:].rearrange("p a r -> p r a"))
+        for t in PRM['dxt']:
+            dx(t, (s_neg, s_neg))
         for gg in range(2):
             dz_quant_half(z, gg)
             for n in range(2):
@@ -377,11 +403,11 @@ def tile_hebbianlayer_pb_v_kernel(tc, prev_act, W1, b1, W2, b2, dopamine, seroto
 
         tags = (("w", 3), ("s", 2), ("dz", 1), ("w", 3), ("s", 2), ("w", 3), ("dz", 1), ("acc", 2))
 
-        def dw(n, engines, tag, bufs):
-            for q in range(4):
-                st = work.tile([P, 2, 512], F32, name="st", tag=tag, bufs=bufs, align_bytes=64)
-                for b in range(2):
-                    d = 2 * q + b
+        def dw(n, engines, tag, bufs, nb):
+            for q in range(8 // nb):
+                st = work.tile([P, nb, 512], F32, name="st", tag=tag, bufs=bufs, align_bytes=64)
+                for b in range(nb):
+                    d = nb * q + b
                     pt, pb = tags[d]
                     ps = psum.tile([P, 512], F32, name="dwp", tag=pt, bufs=pb)
                     nc.tensor.matmul_mx(out=ps[:], lhsT=pv_codes[:, P * d : P * (d + 1)].bitcast(E4), lhsT_scale=pv_scales[:, P * d : P * (d + 1)], rhs=t1_codes[:, 512 * n : 512 * (n + 1)].bitcast(E5), rhs_scale=t1_scales[:, 512 * n : 512 * (n + 1)], start=True, stop=True)
@@ -394,7 +420,7 @@ def tile_hebbianlayer_pb_v_kernel(tc, prev_act, W1, b1, W2, b2, dopamine, seroto
         dz1_transposes(3)
         tok_quant(1)
         dz1_copy(3, nc.vector.tensor_copy)
-        dw(0, (s_neg, s_neg, s_neg, s_neg, s_neg, v_neg, s_neg, v_neg), "h", 5)
+        dw(0, (s_neg, s_neg, s_neg, s_neg, s_neg, v_neg, s_neg, v_neg), "h", 5, 2)
         dz1_quant(3)
-        dw(1, (v_neg, s_neg, v_neg, s_neg, v_neg, s_neg, v_neg, s_neg), "wg", 4)
+        dw(1, (v_neg, s_neg, v_neg, s_neg, v_neg, s_neg, v_neg, s_neg), "wg", 2, 4)
         dx(3, (v_neg, s_neg))

@@ -18,9 +18,9 @@ ALU = mybir.AluOpType
 ACT = mybir.ActivationFunctionType
 
 P = 128
-PRM = {'w_at': {1: [0], 2: [1], 3: [2], 4: [3], 5: [4], 6: [5], 7: [6], 8: [7], 9: [8], 10: [9]}, 'wload': {2: [2], 3: [3], 4: [4], 5: [5], 6: [6], 7: [7], 8: [8], 9: [9]}, 'wfirst': True, 'gstep': 1, 'z1': [5, 8, 10, 14], 'mxa': {3: [(0, 0, 0, 2)], 4: [(0, 0, 2, 4)], 5: [(0, 0, 4, 6)], 6: [(0, 0, 6, 8)], 7: [(0, 1, 0, 2)], 9: [(0, 1, 2, 4), (0, 1, 4, 6), (1, 0, 0, 2)], 10: [(0, 1, 6, 8), (1, 0, 2, 4), (1, 0, 4, 6)], 11: [(1, 0, 6, 8), (1, 1, 0, 2)], 12: [(1, 1, 2, 4), (1, 1, 4, 6), (1, 1, 6, 8), (2, 0, 0, 2), (2, 0, 2, 4)], 13: [(2, 1, 0, 2), (2, 1, 2, 4)], 14: [(2, 0, 4, 6), (2, 1, 4, 6)], 15: [(2, 0, 6, 8), (2, 1, 6, 8), (3, 0, 0, 2), (3, 1, 0, 2)]}, 'mxc': {}, 'mask': {8: [(0, 0)], 10: [(0, 1)], 11: [(1, 0)], 12: [(1, 1)], 15: [(2, 0), (2, 1)]}, 'tr': {11: 0, 14: 1}, 'q': {11: 0, 14: 1}, 'dx': {13: 0, 15: 1}, 'trt': [2], 'qt': [2], 'dxt': [2], 'pesum': [1, 2, 3, 4, 5, 6, 7, 8, 9, 10, 11, 12, 13, 14], 'mxt': [[(3, 0, 2, 4), (3, 1, 2, 4)], [(3, 0, 4, 6), (3, 1, 4, 6)]]}
+PRM = {'w_at': {1: [0], 2: [1], 3: [2], 4: [3], 5: [4], 6: [5], 7: [6], 8: [7], 9: [8], 10: [9]}, 'wload': {0: [2], 2: [3], 3: [4], 4: [5], 5: [6], 6: [7], 7: [8], 8: [9]}, 'wfirst': False, 'gstep': 0, 'z1': [4, 6, 9, 14], 'mxa': {3: [(0, 0, 0, 2)], 5: [(0, 0, 2, 4), (0, 0, 4, 6)], 6: [(0, 0, 6, 8)], 8: [(0, 1, 0, 2), (0, 1, 2, 4)], 9: [(0, 1, 4, 6), (1, 0, 0, 2), (1, 0, 2, 4), (1, 0, 4, 6)], 10: [(0, 1, 6, 8), (1, 0, 6, 8)], 11: [(1, 1, 0, 2), (1, 1, 2, 4), (1, 1, 4, 6), (1, 1, 6, 8)], 12: [(2, 0, 0, 2), (2, 0, 2, 4)], 13: [(2, 0, 4, 6)], 14: [(2, 0, 6, 8), (2, 1, 0, 2), (2, 1, 2, 4)], 15: [(2, 1, 4, 6), (2, 1, 6, 8)]}, 'mxc': {15: [(3, 0, 0, 4), (3, 1, 0, 4)]}, 'mask': {8: [(0, 0)], 10: [(0, 1)], 11: [(1, 0)], 12: [(1, 1)], 14: [(2, 0)], 15: [(2, 1)]}, 'tr': {12: 0, 13: 1}, 'q': {12: 0, 14: 1}, 'dx': {13: 0, 15: 1}, 'trt': [2], 'qt': [2], 'dxt': [2], 'pesum': [1, 2, 3, 4, 5, 6, 7, 8, 9, 10, 11, 12, 13, 14], 'mxt': [[], [(3, 0, 4, 6), (3, 1, 4, 6)]]}
 J = 256
-SPLIT = 192
+SPLIT = 176
 NCH = B * E // (P * J)
 
 
@@ -33,6 +33,7 @@ def tile_hebbianlayer_pb_v_kernel(tc, prev_act, W1, b1, W2, b2, dopamine, seroto
     w2_v = W2.rearrange("(n b r) k -> r n b k", n=2, b=4)
     w1_v = W1.rearrange("(n b r) k -> r n b k", n=2, b=4)
     o0_v = out_0.rearrange("(p j) d -> p j d", j=4)
+    o1_v = out_1.rearrange("(b p) n -> p b n", p=P)
 
     with ExitStack() as ctx:
         keep = ctx.enter_context(tc.tile_pool(name="keep", bufs=1))
@@ -205,7 +206,7 @@ def tile_hebbianlayer_pb_v_kernel(tc, prev_act, W1, b1, W2, b2, dopamine, seroto
 
         def mm_dhid(t, n, g):
             if g == 0:
-                acc[t, n] = psum.tile([P, 512], F32, name="acc", tag="w" if t == 3 else "acc", bufs=3 if t == 3 else 2)
+                acc[t, n] = psum.tile([P, 512], F32, name="acc", tag="s" if t == 3 else "acc", bufs=2)
             nc.tensor.matmul_mx(out=acc[t, n][:], lhsT=dz2c[t][:, g, :].bitcast(E5), lhsT_scale=dz2s[t][:, g, :], rhs=w2_codes[n][:, g, :].bitcast(E4), rhs_scale=w2_scales[n][:, g, :], start=(g == 0), stop=(g == 7))
 
         def v_mask(t, n):
@@ -367,23 +368,20 @@ def tile_hebbianlayer_pb_v_kernel(tc, prev_act, W1, b1, W2, b2, dopamine, seroto
         dz_transposes(z - 1)
         dz_copy(z - 1)
         v_d1(z)
-        mx_list(PRM['mxt'][0])
         for t in PRM['trt']:
             dz1_transposes(t)
             dz1_copy(t, nc.scalar.copy)
-        dz_quant(z - 1)
-        mx_list(PRM['mxt'][1])
         v_o_half(z, 0)
         h0 = dz_half(z, 0)
         v_o_half(z, 1)
         h1 = dz_half(z, 1)
+        dz_quant(z - 1)
+        mx_list(PRM['mxt'][1])
         for t in PRM['qt']:
             dz1_quant(t)
         dzg[z] = work.tile([P, 2, P, 4], BF16, name="dzg", tag="dzg", bufs=2, align_bytes=64)
         nc.scalar.copy(dzg[z][:, 0, :, :].bitcast(F32), h0[:].rearrange("p a r -> p r a"))
         nc.vector.tensor_copy(out=dzg[z][:, 1, :, :].bitcast(F32), in_=h1[:].rearrange("p a r -> p r a"))
-        for t in PRM['dxt']:
-            dx(t, (s_neg, s_neg))
         for gg in range(2):
             dz_quant_half(z, gg)
             for n in range(2):
@@ -396,31 +394,39 @@ def tile_hebbianlayer_pb_v_kernel(tc, prev_act, W1, b1, W2, b2, dopamine, seroto
         v_mask(3, 0)
         tok_copy(nc.scalar.copy, 0, SPLIT)
         tok_copy(nc.vector.tensor_copy, SPLIT, 512)
+        for t in PRM['dxt']:
+            dx(t, (s_neg, s_neg))
 
         def tok_quant(n):
             cols = slice(512 * n, 512 * (n + 1))
             nc.vector.quantize_mx(out=t1_codes[:, cols].bitcast(E5), scales=t1_scales[:, cols], in_=tok[:, cols, :].rearrange("p d j -> p (d j)"))
 
-        tags = (("w", 3), ("s", 2), ("dz", 1), ("w", 3), ("s", 2), ("w", 3), ("dz", 1), ("acc", 2))
+        tags = (("acc", 2), ("dz", 1), ("acc", 2), ("w", 3), ("w", 3), ("s", 2), ("w", 3), ("s", 2))
 
-        def dw(n, engines, tag, bufs, nb):
-            for q in range(8 // nb):
-                st = work.tile([P, nb, 512], F32, name="st", tag=tag, bufs=bufs, align_bytes=64)
-                for b in range(nb):
-                    d = nb * q + b
+        def dw(n, engines, tag, bufs, nb, groups):
+            d = 0
+            st = None
+            for size in groups:
+                if st is None or used + size > nb:
+                    st = work.tile([P, nb, 512], F32, name="st", tag=tag, bufs=bufs, align_bytes=64)
+                    used = 0
+                d0 = d
+                for b in range(used, used + size):
                     pt, pb = tags[d]
                     ps = psum.tile([P, 512], F32, name="dwp", tag=pt, bufs=pb)
                     nc.tensor.matmul_mx(out=ps[:], lhsT=pv_codes[:, P * d : P * (d + 1)].bitcast(E4), lhsT_scale=pv_scales[:, P * d : P * (d + 1)], rhs=t1_codes[:, 512 * n : 512 * (n + 1)].bitcast(E5), rhs_scale=t1_scales[:, 512 * n : 512 * (n + 1)], start=True, stop=True)
                     engines[d](st[:, b, :], ps[:])
-                    nc.sync.dma_start(out=out_1[P * d : P * (d + 1), 512 * n : 512 * (n + 1)], in_=st[:, b, :])
+                    d += 1
+                nc.sync.dma_start(out=o1_v[:, d0:d, 512 * n : 512 * (n + 1)], in_=st[:, used : used + size, :])
+                used += size
 
         tok_quant(0)
         v_mask(3, 1)
+        dw(0, (s_neg,) * 8, "h", 5, 2, (1, 1, 2, 2, 2))
         tok_copy(nc.vector.tensor_copy, 512, 1024)
         dz1_transposes(3)
         tok_quant(1)
         dz1_copy(3, nc.vector.tensor_copy)
-        dw(0, (s_neg, s_neg, s_neg, s_neg, s_neg, v_neg, s_neg, v_neg), "h", 5, 2)
+        dw(1, (v_neg, s_neg) * 4, "wg", 2, 4, (2, 2, 2, 2))
         dz1_quant(3)
-        dw(1, (v_neg, s_neg, v_neg, s_neg, v_neg, s_neg, v_neg, s_neg), "wg", 2, 4)
         dx(3, (v_neg, s_neg))

@@ -133,26 +133,26 @@ def tile_hebbianlayer_pb_v_kernel(tc, prev_act, W1, b1, W2, b2, dopamine, seroto
             return xs[i][:].rearrange("p (r a) j -> p a j r", r=2)[:, :, :, ::-1]
 
         def v_y(i):
-            ys[i] = work.tile([P, 4, J], F32, name="y", tag="y", bufs=2, align_bytes=64)
-            nc.vector.tensor_tensor(out=ys[i][:].rearrange("p (a e) j -> p a j e", e=2), in0=hs[i][:].rearrange("p j (a e) -> p a j e", e=2), in1=x_pairs(i), op=ALU.mult)
+            ys[i] = work.tile([P, 2, J, 2], F32, name="y", tag="y", bufs=2, align_bytes=64)
+            nc.vector.tensor_tensor(out=ys[i][:], in0=hs[i][:].rearrange("p j (a e) -> p a j e", e=2), in1=x_pairs(i), op=ALU.mult)
 
         def pe_s(i):
             ss[i] = psum.tile([P, J], F32, name="s", tag="s", bufs=2)
             pe_s_part(i, 0)
 
         def pe_s_part(i, c):
-            nc.tensor.matmul(ss[i][:], lhsT=ident_f[:], rhs=ys[i][:, c, :], start=(c == 0), stop=(c == 3))
+            nc.tensor.matmul(ss[i][:], lhsT=ident_f[:], rhs=ys[i][:, c // 2, :, c % 2], start=(c == 0), stop=(c == 3))
 
         def v_s1(i):
             ss[i] = work.tile([P, J], F32, name="s1", tag="s1", bufs=1, align_bytes=64)
-            nc.vector.tensor_tensor(out=ss[i][:], in0=ys[i][:, 0, :], in1=ys[i][:, 2, :], op=ALU.add)
+            nc.vector.tensor_tensor(out=ss[i][:], in0=ys[i][:, 0, :, 0], in1=ys[i][:, 1, :, 0], op=ALU.add)
 
         def v_s2(i):
-            nc.vector.tensor_tensor(out=ss[i][:], in0=ss[i][:], in1=ys[i][:, 3, :], op=ALU.add)
+            nc.vector.tensor_tensor(out=ss[i][:], in0=ss[i][:], in1=ys[i][:, 1, :, 1], op=ALU.add)
 
         def v_t(i):
             ts[i] = work.tile([P, J], F32, name="t", tag="t", bufs=2, align_bytes=64)
-            nc.vector.tensor_tensor(out=ts[i][:], in0=ys[i][:, 1, :], in1=ss[i][:], op=ALU.mult)
+            nc.vector.tensor_tensor(out=ts[i][:], in0=ys[i][:, 0, :, 1], in1=ss[i][:], op=ALU.mult)
 
         def v_d1(i):
             nc.vector.tensor_tensor(out=xs[i][:, 0, :], in0=g_part(i)[:, 0, :], in1=ts[i][:], op=ALU.subtract)

from contextlib import ExitStack

import concourse.mybir as mybir
from concourse.masks import make_identity

B, D, E, NM = 512, 1024, 1024, 4

FLOPS = 2 * B * D * NM * E + 2 * (2 * B * D * D)
BYTES = 2 * (B * D + D * D + D * NM * E + NM * B * E) + 4 * (B * D + B * NM * E + B * D + D * D)

F32 = mybir.dt.float32
BF16 = mybir.dt.bfloat16
U32 = mybir.dt.uint32
U8 = mybir.dt.uint8
E4 = mybir.dt.float8_e4m3fn_x4
E5 = mybir.dt.float8_e5m2_x4
ALU = mybir.AluOpType
ACT = mybir.ActivationFunctionType

P = 128
PRM = {'w_at': {1: [0], 2: [1], 3: [2], 4: [3], 5: [4], 6: [5], 7: [6], 8: [7], 9: [8], 10: [9]}, 'wload': {0: [2], 2: [3], 3: [4], 4: [5], 5: [6], 6: [7], 7: [8], 8: [9]}, 'wfirst': False, 'gstep': 0, 'z1': [4, 6, 9, 14], 'mxa': {3: [(0, 0, 0, 2)], 5: [(0, 0, 2, 4), (0, 0, 4, 6)], 6: [(0, 0, 6, 8)], 8: [(0, 1, 0, 2), (0, 1, 2, 4)], 9: [(0, 1, 4, 6), (1, 0, 0, 2), (1, 0, 2, 4), (1, 0, 4, 6)], 10: [(0, 1, 6, 8), (1, 0, 6, 8)], 11: [(1, 1, 0, 2), (1, 1, 2, 4), (1, 1, 4, 6), (1, 1, 6, 8)], 12: [(2, 0, 0, 2), (2, 0, 2, 4)], 13: [(2, 0, 4, 6)], 14: [(2, 0, 6, 8), (2, 1, 0, 2), (2, 1, 2, 4)], 15: [(2, 1, 4, 6), (2, 1, 6, 8)]}, 'mxc': {15: [(3, 0, 0, 4), (3, 1, 0, 4)]}, 'mask': {8: [(0, 0)], 10: [(0, 1)], 11: [(1, 0)], 12: [(1, 1)], 14: [(2, 0)], 15: [(2, 1)]}, 'tr': {12: 0, 13: 1}, 'q': {12: 0, 14: 1}, 'dx': {13: 0, 15: 1}, 'trt': [2], 'qt': [2], 'dxt': [2], 'pesum': [1, 2, 3, 4, 5, 6, 7, 8, 9, 10, 11, 12, 13, 14], 'mxt': [[], [(3, 0, 4, 6), (3, 1, 4, 6)]]}
J = 256
SPLIT = 176
NCH = B * E // (P * J)


def tile_hebbianlayer_pb_v_kernel(tc, prev_act, W1, b1, W2, b2, dopamine, serotonin, glutamate, gaba, z1, h, grad_out, out_0, out_1):
    nc = tc.nc
    prev_v = prev_act.rearrange("(p j) d -> p j d", j=4)
    h_v = h.rearrange("(p j) k -> p j k", j=4)
    z1_v = z1.rearrange("(p j) d -> p j d", j=4)
    g_v = grad_out.rearrange("(a e p j) u -> p a e j u", a=2, e=2, j=4)
    w2_v = W2.rearrange("(n b r) k -> r n b k", n=2, b=4)
    w1_v = W1.rearrange("(n b r) k -> r n b k", n=2, b=4)
    o0_v = out_0.rearrange("(p j) d -> p j d", j=4)
    o1_v = out_1.rearrange("(b p) n -> p b n", p=P)

    with ExitStack() as ctx:
        keep = ctx.enter_context(tc.tile_pool(name="keep", bufs=1))
        work = ctx.enter_context(tc.tile_pool(name="work", bufs=2))
        psum = ctx.enter_context(tc.psum_pool(name="psum", bufs=2))
        ctx.enter_context(tc.manual_schedule())

        ident_f = keep.tile([P, P], F32, name="ident_f")
        eps = keep.tile([P, 1], F32, name="eps")
        warm = keep.tile([P, 1], F32, name="warm")
        nc.vector.memset(eps[:], 1e-25)
        make_identity(nc, ident_f[:])
        nc.scalar.activation(warm[:], eps[:], ACT.Abs_reciprocal_sqrt)

        w2_codes = [keep.tile([P, 8, 512], U32, name="w2c%d" % n, align_bytes=64) for n in range(2)]
        w2_scales = [keep.tile([P, 8, 512], U8, name="w2s%d" % n, align_bytes=64) for n in range(2)]
        w1_codes = [keep.tile([P, 2, 512], U32, name="w1c%d" % n, align_bytes=64) for n in range(2)]
        w1_scales = [keep.tile([P, 2, 512], U8, name="w1s%d" % n, align_bytes=64) for n in range(2)]
        pv_codes = keep.tile([P, D], U32, name="pv_codes", align_bytes=64)
        pv_scales = keep.tile([P, D], U8, name="pv_scales", align_bytes=64)
        dz1 = keep.tile([P, 4, D], BF16, name="dz1", align_bytes=64)
        t1_codes = keep.tile([P, D], U32, name="t1_codes", align_bytes=64)
        t1_scales = keep.tile([P, D], U8, name="t1_scales", align_bytes=64)

        hs, gs, ws, z1s = {}, {}, {}, {}
        h2s, invs, inv2s, xs, ys, ss, ts, os_ = {}, {}, {}, {}, {}, {}, {}, {}
        wg, dzg, dzx, dz2c, dz2s, acc, d1c, d1x, d1g = {}, {}, {}, {}, {}, {}, {}, {}, {}

        def load_h(i):
            if i < NCH:
                hs[i] = work.tile([P, J, 4], F32, name="h", tag="h", bufs=5, align_bytes=64)
                nc.sync.dma_start(out=hs[i][:].rearrange("p j c -> p (j c)"), in_=h_v[:, i // 4, (i % 4) * 4 * J : (i % 4 + 1) * 4 * J])

        def load_g(t, lo=0, hi=E):
            if t > 3:
                return
            if lo == 0:
                gs[t] = work.tile([P, 4, E], BF16, name="g", tag="g", bufs=2, align_bytes=64)
            planes = gs[t][:].rearrange("p (r a) u -> p r a u", r=2)
            for e in range(2):
                nc.sync.dma_start(out=planes[:, 1 - e, :, lo:hi], in_=g_v[:, :, e, t, lo:hi])

        def load_w(k):
            if k < 10:
                ws[k] = work.tile([P, 4, 1024], BF16, name="wraw", tag="wraw", bufs=3, align_bytes=64)
                src = w2_v[:, k // 4, :, (k % 4) * 1024 : (k % 4 + 1) * 1024] if k < 8 else w1_v[:, k - 8, :, :]
                nc.sync.dma_start(out=ws[k][:], in_=src)

        def load_z1(t):
            z1s[t] = work.tile([P, D], F32, name="z1t", tag="z1t", bufs=2, align_bytes=64)
            nc.sync.dma_start(out=z1s[t][:], in_=z1_v[:, t, :])

        def w_transposes(k, gg, half):
            xt = psum.tile([P, 2, 2, P], F32, name="xt", tag="w", bufs=3)
            words = ws[k][:].bitcast(F32)
            for bb in range(2):
                for u in range(2):
                    nc.tensor.transpose(xt[:, bb, u, :], words[:, 2 * half + bb, 256 * gg + u : 256 * (gg + 1) : 2], ident_f[:])
            return xt

        def w_copy(k, gg, half, xt):
            if gg == 0 and half == 0:
                wg[k] = work.tile([P, 2, 4, P, 4], BF16, name="wg", tag="wg", bufs=2, align_bytes=64)
            dst = wg[k][:].bitcast(F32)
            nc.scalar.copy(dst[:, gg, 2 * half : 2 * half + 2, :, :], xt[:].rearrange("p b u r -> p b r u"))

        def w_quant(k):
            if k < 8:
                g, co, sc = 2 * (k % 4), w2_codes[k // 4], w2_scales[k // 4]
            else:
                g, co, sc = 0, w1_codes[k - 8], w1_scales[k - 8]
            nc.vector.quantize_mx(out=co[:, g : g + 2, :].rearrange("p g n -> p (g n)").bitcast(E4), scales=sc[:, g : g + 2, :].rearrange("p g n -> p (g n)"), in_=wg[k][:].rearrange("p g b r t -> p (g b r t)"))

        def sc_square(i):
            h2s[i] = work.tile([P, 2, J, 2], F32, name="h2", tag="h2", bufs=4, align_bytes=64)
            nc.scalar.activation(h2s[i][:].rearrange("p a j e -> p j a e"), hs[i][:].rearrange("p j (a e) -> p j a e", e=2), ACT.Square)

        def sc_inv(i, src=None):
            invs[i] = work.tile([P, J], F32, name="inv", tag="inv", bufs=2, align_bytes=64)
            nc.scalar.activation(invs[i][:], h2s[i][:, 0, :, 1] if src is None else src, ACT.Abs_reciprocal_sqrt, bias=eps[:])

        def sc_inv2(i):
            inv2s[i] = work.tile([P, J], F32, name="inv2", tag="inv2", bufs=2, align_bytes=64)
            nc.scalar.activation(inv2s[i][:], invs[i][:], ACT.Square)

        def g_part(i):
            return gs[i // 4][:, :, (i % 4) * J : (i % 4 + 1) * J]

        def v_x(i):
            xs[i] = work.tile([P, 4, J], F32, name="x", tag="x", bufs=3, align_bytes=64)
            nc.vector.scalar_tensor_tensor(out=xs[i][:, 1:4, :], in0=invs[i][:].unsqueeze(1).to_broadcast([P, 3, J]), scalar=1e6, in1=g_part(i)[:, 1:4, :], op0=ALU.min, op1=ALU.mult)

        def v_m(i):
            nc.vector.scalar_tensor_tensor(out=xs[i][:, 0, :], in0=invs[i][:], scalar=1e6, in1=inv2s[i][:], op0=ALU.is_lt, op1=ALU.mult)

        def x_pairs(i):
            return xs[i][:].rearrange("p (r a) j -> p a j r", r=2)[:, :, :, ::-1]

        def v_y(i):
            ys[i] = work.tile([P, 2, J, 2], F32, name="y", tag="y", bufs=2, align_bytes=64)
            nc.vector.tensor_tensor(out=ys[i][:], in0=hs[i][:].rearrange("p j (a e) -> p a j e", e=2), in1=x_pairs(i), op=ALU.mult)

        def pe_s(i):
            ss[i] = psum.tile([P, J], F32, name="s", tag="s", bufs=2)
            pe_s_part(i, 0)

        def pe_s_part(i, c):
            nc.tensor.matmul(ss[i][:], lhsT=ident_f[:], rhs=ys[i][:, c // 2, :, c % 2], start=(c == 0), stop=(c == 3))

        def v_s1(i):
            ss[i] = work.tile([P, J], F32, name="s1", tag="s1", bufs=1, align_bytes=64)
            nc.vector.tensor_tensor(out=ss[i][:], in0=ys[i][:, 0, :, 0], in1=ys[i][:, 1, :, 0], op=ALU.add)

        def v_s2(i):
            nc.vector.tensor_tensor(out=ss[i][:], in0=ss[i][:], in1=ys[i][:, 1, :, 1], op=ALU.add)

        def v_t(i):
            ts[i] = work.tile([P, J], F32, name="t", tag="t", bufs=2, align_bytes=64)
            nc.vector.tensor_tensor(out=ts[i][:], in0=ys[i][:, 0, :, 1], in1=ss[i][:], op=ALU.mult)

        def v_d1(i):
            nc.vector.tensor_tensor(out=xs[i][:, 0, :], in0=g_part(i)[:, 0, :], in1=ts[i][:], op=ALU.subtract)

        def v_o(i):
            os_[i] = work.tile([P, 2, J, 2], BF16, name="o", tag="o", bufs=2, align_bytes=64)
            xp = xs[i][:].rearrange("p (r a) j -> p (a j) r", r=2)[:, :, ::-1]
            nc.vector.scalar_tensor_tensor(out=os_[i][:].rearrange("p a j e -> p (a j) e"), in0=h2s[i][:].rearrange("p a j e -> p (a j) e"), scalar=1.0, in1=xp, op0=ALU.subtract, op1=ALU.mult)

        def v_o_half(i, gg):
            if gg == 0:
                os_[i] = work.tile([P, 2, J, 2], BF16, name="o", tag="o", bufs=2, align_bytes=64)
            cols = slice(P * gg, P * (gg + 1))
            xp = x_pairs(i)
            for a in range(2):
                nc.vector.scalar_tensor_tensor(out=os_[i][:, a, cols, :], in0=h2s[i][:, a, cols, :], scalar=1.0, in1=xp[:, a, cols, :], op0=ALU.subtract, op1=ALU.mult)

        def dz_half(i, gg):
            xt = psum.tile([P, 2, P], F32, name="dzh", tag="w", bufs=3)
            words = os_[i][:].rearrange("p a j e -> p (a j e)").bitcast(F32)
            for a in range(2):
                nc.tensor.transpose(xt[:, a, :], words[:, a * J + gg * P : a * J + (gg + 1) * P], ident_f[:])
            return xt

        def dz_quant_half(i, gg):
            t, g = i // 4, 2 * (i % 4) + gg
            nc.vector.quantize_mx(out=dz2c[t][:, g, :].bitcast(E5), scales=dz2s[t][:, g, :], in_=dzg[i][:, gg, :, :].rearrange("p r t -> p (r t)"))

        def dz_transposes(i):
            xt = psum.tile([P, 2, 2, P], F32, name="dzt", tag="dz", bufs=1)
            words = os_[i][:].rearrange("p a j e -> p (a j e)").bitcast(F32)
            for gg in range(2):
                for a in range(2):
                    nc.tensor.transpose(xt[:, gg, a, :], words[:, a * J + gg * P : a * J + (gg + 1) * P], ident_f[:])
            dzx[i] = xt

        def dz_copy(i):
            dzg[i] = work.tile([P, 2, P, 4], BF16, name="dzg", tag="dzg", bufs=2, align_bytes=64)
            nc.scalar.copy(dzg[i][:].bitcast(F32), dzx[i][:].rearrange("p g a r -> p g r a"))

        def dz_quant(i):
            t, u = i // 4, i % 4
            if u == 0:
                dz2c[t] = work.tile([P, 8, P], U32, name="dz2c", tag="dz2c", bufs=2, align_bytes=64)
                dz2s[t] = work.tile([P, 8, P], U8, name="dz2s", tag="dz2s", bufs=2, align_bytes=64)
            nc.vector.quantize_mx(
                out=dz2c[t][:, 2 * u : 2 * u + 2, :].rearrange("p g r -> p (g r)").bitcast(E5),
                scales=dz2s[t][:, 2 * u : 2 * u + 2, :].rearrange("p g r -> p (g r)"),
                in_=dzg[i][:].rearrange("p g r t -> p (g r t)"),
            )

        def mm_dhid(t, n, g):
            if g == 0:
                acc[t, n] = psum.tile([P, 512], F32, name="acc", tag="s" if t == 3 else "acc", bufs=2)
            nc.tensor.matmul_mx(out=acc[t, n][:], lhsT=dz2c[t][:, g, :].bitcast(E5), lhsT_scale=dz2s[t][:, g, :], rhs=w2_codes[n][:, g, :].bitcast(E4), rhs_scale=w2_scales[n][:, g, :], start=(g == 0), stop=(g == 7))

        def v_mask(t, n):
            nc.vector.scalar_tensor_tensor(out=dz1[:, t, 512 * n : 512 * (n + 1)], in0=z1s[t][:, 512 * n : 512 * (n + 1)], scalar=0.0, in1=acc[t, n][:], op0=ALU.is_gt, op1=ALU.mult)

        def dz1_transposes(t):
            d1x[t] = psum.tile([P, 2, 2, P], F32, name="d1t", tag="w", bufs=3)
            words = dz1[:, t, :].bitcast(F32)
            for g in range(2):
                for u in range(2):
                    nc.tensor.transpose(d1x[t][:, g, u, :], words[:, 256 * g + u : 256 * (g + 1) : 2], ident_f[:])

        def dz1_copy(t, copy):
            d1g[t] = work.tile([P, 2, P, 4], BF16, name="d1g", tag="d1g", bufs=1, align_bytes=64)
            copy(d1g[t][:].bitcast(F32), d1x[t][:].rearrange("p g u r -> p g r u"))

        def dz1_quant(t):
            co = work.tile([P, 2, P], U32, name="d1c", tag="d1c", bufs=2, align_bytes=64)
            sc = work.tile([P, 2, P], U8, name="d1s", tag="d1s", bufs=2, align_bytes=64)
            nc.vector.quantize_mx(out=co[:].rearrange("p g r -> p (g r)").bitcast(E5), scales=sc[:].rearrange("p g r -> p (g r)"), in_=d1g[t][:].rearrange("p g r t -> p (g r t)"))
            d1c[t] = (co, sc)

        def s_neg(dst, src):
            nc.scalar.activation(dst, src, ACT.Copy, scale=-1.0)

        def v_neg(dst, src):
            nc.vector.tensor_scalar(out=dst, in0=src, scalar1=-1.0, scalar2=None, op0=ALU.mult)

        def dx(t, engines):
            co, sc = d1c[t]
            ost = work.tile([P, D], F32, name="ost", tag="ost", bufs=2, align_bytes=64)
            for n in range(2):
                ps = psum.tile([P, 512], F32, name="dxp", tag="w", bufs=3)
                for g in range(2):
                    nc.tensor.matmul_mx(out=ps[:], lhsT=co[:, g, :].bitcast(E5), lhsT_scale=sc[:, g, :], rhs=w1_codes[n][:, g, :].bitcast(E4), rhs_scale=w1_scales[n][:, g, :], start=(g == 0), stop=(g == 1))
                engines[n](ost[:, 512 * n : 512 * (n + 1)], ps[:])
            nc.sync.dma_start(out=o0_v[:, t, :], in_=ost[:])

        pv = work.tile([P, 4, 1024], BF16, name="wraw", tag="wraw", bufs=3, align_bytes=64)
        def load_pv(k):
            nc.sync.dma_start(out=pv[:, :, 512 * k : 512 * (k + 1)], in_=prev_v[:, :, 512 * k : 512 * (k + 1)])

        load_pv(0)
        load_h(0)
        load_g(0, 0, 512)
        load_h(1)
        load_pv(1)
        load_h(2)
        load_w(0)
        load_g(0, 512, 1024)
        load_h(3)
        load_w(1)

        pvg = work.tile([P, D, 4], BF16, name="tok", tag="tok", bufs=1, align_bytes=64)

        def pv_copy(k):
            cols = slice(512 * k, 512 * (k + 1))
            nc.vector.tensor_copy(out=pvg[:, cols, :], in_=pv[:, :, cols].rearrange("p j d -> p d j"))

        def pv_quant(k):
            cols = slice(512 * k, 512 * (k + 1))
            nc.vector.quantize_mx(out=pv_codes[:, cols].bitcast(E4), scales=pv_scales[:, cols], in_=pvg[:, cols, :].rearrange("p d j -> p (d j)"))

        pv_copy(0)
        sq = keep.tile([P, J], F32, name="sq")
        nc.scalar.activation(sq[:], hs[0][:, :, 1], ACT.Square)
        sc_inv(0, sq[:])
        sc_square(0)
        sc_inv2(0)
        sc_square(1)
        sc_inv(1)
        sc_inv2(1)
        pv_quant(0)
        v_x(0)
        v_m(0)

        def mx_list(lst):
            for t, n, g0, g1 in lst:
                for g in range(g0, g1):
                    mm_dhid(t, n, g)

        mx_a, mx_c, mask_at, t_at, q_at, dx_at, pe_sum = PRM['mxa'], PRM['mxc'], PRM['mask'], PRM['tr'], PRM['q'], PRM['dx'], PRM['pesum']
        for i in range(NCH):
            last = i == NCH - 1
            pieces = PRM['w_at'].get(i, ())
            units = [(k, gg, half) for k in pieces for gg in range(2) for half in range(2)]
            cut1, cut2 = (2, 3) if len(units) == 4 else (3, 6)
            for k in PRM['wload'].get(i, ()) if PRM['wfirst'] else ():
                load_w(k)
            load_h(i + 4)
            for k in PRM['wload'].get(i, ()) if not PRM['wfirst'] else ():
                load_w(k)
            if i % 4 == PRM['gstep']:
                load_g(i // 4 + 1)
            if i in PRM['z1']:
                load_z1(PRM['z1'].index(i))

            if i + 2 < NCH:
                sc_square(i + 2)
            if i >= 2:
                dz_transposes(i - 2)
                dz_copy(i - 2)
            if i + 2 < NCH:
                sc_inv(i + 2)
            v_y(i)
            mx_list(mx_a.get(i, ()))
            for k, gg, half in units[:1]:
                w_copy(k, gg, half, w_transposes(k, gg, half))
            if i + 2 < NCH:
                sc_inv2(i + 2)
            if i in t_at:
                dz1_transposes(t_at[i])
                dz1_copy(t_at[i], nc.scalar.copy)
            for k, gg, half in units[1:cut1]:
                w_copy(k, gg, half, w_transposes(k, gg, half))
            if i in pe_sum:
                pe_s(i)
            for k, gg, half in units[cut1:cut2]:
                w_copy(k, gg, half, w_transposes(k, gg, half))
            if i in pe_sum:
                pe_s_part(i, 2)
            for k, gg, half in units[cut2:]:
                w_copy(k, gg, half, w_transposes(k, gg, half))
            if i in pe_sum:
                pe_s_part(i, 3)
            if i in dx_at:
                dx(dx_at[i], (s_neg, s_neg))
            if i == 0:
                pv_copy(1)
            if not last:
                v_x(i + 1)
            if i == 0:
                pv_quant(1)
            if i >= 1 and i - 1 in pe_sum:
                v_t(i - 1)
            if i not in pe_sum:
                v_s1(i)
            if not last:
                v_m(i + 1)
            if i >= 1:
                v_d1(i - 1)
            for k in PRM['w_at'].get(i - 1, ()):
                w_quant(k)
            if i not in pe_sum:
                v_s2(i)
            if i >= 2:
                dz_quant(i - 2)
            if i >= 1:
                v_o(i - 1)
            if i not in pe_sum:
                v_t(i)
            for t, n in mask_at.get(i, ()):
                v_mask(t, n)
            if i in q_at:
                dz1_quant(q_at[i])
            mx_list(mx_c.get(i, ()))

        z = NCH - 1
        dz_transposes(z - 1)
        dz_copy(z - 1)
        v_d1(z)
        for t in PRM['trt']:
            dz1_transposes(t)
            dz1_copy(t, nc.scalar.copy)
        v_o_half(z, 0)
        h0 = dz_half(z, 0)
        v_o_half(z, 1)
        h1 = dz_half(z, 1)
        dz_quant(z - 1)
        mx_list(PRM['mxt'][1])
        for t in PRM['qt']:
            dz1_quant(t)
        dzg[z] = work.tile([P, 2, P, 4], BF16, name="dzg", tag="dzg", bufs=2, align_bytes=64)
        nc.scalar.copy(dzg[z][:, 0, :, :].bitcast(F32), h0[:].rearrange("p a r -> p r a"))
        nc.vector.tensor_copy(out=dzg[z][:, 1, :, :].bitcast(F32), in_=h1[:].rearrange("p a r -> p r a"))
        for gg in range(2):
            dz_quant_half(z, gg)
            for n in range(2):
                mm_dhid(3, n, 6 + gg)
        tok = work.tile([P, D, 4], BF16, name="tok", tag="tok", bufs=1, align_bytes=64)

        def tok_copy(copy, lo, hi):
            copy(tok[:, lo:hi, :], dz1[:, :, lo:hi].rearrange("p j d -> p d j"))

        v_mask(3, 0)
        tok_copy(nc.scalar.copy, 0, SPLIT)
        tok_copy(nc.vector.tensor_copy, SPLIT, 512)
        for t in PRM['dxt']:
            dx(t, (s_neg, s_neg))

        def tok_quant(n):
            cols = slice(512 * n, 512 * (n + 1))
            nc.vector.quantize_mx(out=t1_codes[:, cols].bitcast(E5), scales=t1_scales[:, cols], in_=tok[:, cols, :].rearrange("p d j -> p (d j)"))

        tags = (("acc", 2), ("dz", 1), ("acc", 2), ("w", 3), ("w", 3), ("s", 2), ("w", 3), ("s", 2))

        def dw(n, engines, tag, bufs, nb, groups):
            d = 0
            st = None
            for size in groups:
                if st is None or used + size > nb:
                    st = work.tile([P, nb, 512], F32, name="st", tag=tag, bufs=bufs, align_bytes=64)
                    used = 0
                d0 = d
                for b in range(used, used + size):
                    pt, pb = tags[d]
                    ps = psum.tile([P, 512], F32, name="dwp", tag=pt, bufs=pb)
                    nc.tensor.matmul_mx(out=ps[:], lhsT=pv_codes[:, P * d : P * (d + 1)].bitcast(E4), lhsT_scale=pv_scales[:, P * d : P * (d + 1)], rhs=t1_codes[:, 512 * n : 512 * (n + 1)].bitcast(E5), rhs_scale=t1_scales[:, 512 * n : 512 * (n + 1)], start=True, stop=True)
                    engines[d](st[:, b, :], ps[:])
                    d += 1
                nc.sync.dma_start(out=o1_v[:, d0:d, 512 * n : 512 * (n + 1)], in_=st[:, used : used + size, :])
                used += size

        tok_quant(0)
        v_mask(3, 1)
        dw(0, (s_neg,) * 8, "h", 5, 2, (1, 1, 2, 2, 2))
        tok_copy(nc.vector.tensor_copy, 512, 1024)
        dz1_transposes(3)
        tok_quant(1)
        dz1_copy(3, nc.vector.tensor_copy)
        dw(1, (v_neg, s_neg) * 4, "wg", 2, 4, (2, 2, 2, 2))
        dz1_quant(3)
        dx(3, (v_neg, s_neg))
